import numpy as np
import ml_dtypes


def mxq(x, axis, fmt="e4m3"):
    dtype, down = {"e4m3": (ml_dtypes.float8_e4m3fn, 7), "e5m2": (ml_dtypes.float8_e5m2, 14)}[fmt]
    v = np.moveaxis(np.asarray(x, np.float32).astype(ml_dtypes.bfloat16).astype(np.float64), axis, -1)
    blocks = v.reshape(v.shape[:-1] + (-1, 32))
    amax = np.abs(blocks).max(-1, keepdims=True)
    byte = np.maximum(np.where(amax > 0, np.frexp(amax)[1] - 1 + 127, 0) - down, 1)
    scale = np.exp2(byte - 127.0)
    codes = (blocks / scale).astype(np.float32).astype(dtype).astype(np.float64)
    return np.moveaxis((codes * scale).reshape(v.shape), -1, axis)


WIDE = False


def mx_kscale(k):
    if not WIDE:
        return np.ones(k)
    levels = np.array([10, -10, 5, -5, 0])
    if k % 512:
        return np.exp2(np.random.permutation(np.resize(levels, k // 32))).repeat(32)
    a = np.empty((k // 512, 16))
    for p in range(k // 512):
        a[p, :8] = np.random.permutation(np.resize(levels, 8))
        for g in range(8):
            far = levels[np.abs(levels - a[p, g]) >= 10]
            a[p, g + 8] = far[np.random.randint(len(far))]
    return np.exp2(a.ravel()).repeat(32)


BF16 = ml_dtypes.bfloat16


def bf(x):
    return np.asarray(x, np.float32).astype(BF16)


def f64(x):
    return np.asarray(x).astype(np.float64)


B, S, D, E, F = 4, 64, 2048, 2048, 4096
EPS = 1e-5


def layernorm(x, g, b):
    m = x.mean(-1, keepdims=True)
    v = ((x - m) ** 2).mean(-1, keepdims=True)
    return (x - m) * (1.0 / np.sqrt(v + EPS)) * g + b


def rotate_half(x):
    return np.concatenate([-x[..., ::2], x[..., 1::2]], axis=-1)


def sinu_pos_emb(dim, length):
    inv_freq = 1.0 / 10000.0 ** (np.arange(0, dim, 2) / dim)
    sp = np.arange(length)[:, None] * inv_freq[None, :]
    return np.concatenate([np.sin(sp), np.cos(sp)], axis=-1)


def setup_inputs():
    s = mx_kscale(D)
    return {"src": bf(np.random.standard_normal((B, S, D)) + 0.5),
            "Wqkv": bf(np.random.standard_normal((3 * E, D)) / np.sqrt(D) / s[None, :]),
            "bqkv": bf(0.1 * np.random.standard_normal(3 * E)),
            "g1": bf((1.0 + 0.1 * np.random.standard_normal(D)) * s),
            "be1": bf(0.1 * np.random.standard_normal(D) * s)}


def reference(src, Wqkv, bqkv, g1, be1):
    xn = layernorm(f64(src), f64(g1), f64(be1))
    qkv = (mxq(xn, 2, "e4m3") @ mxq(f64(Wqkv), 1, "e4m3").T) + f64(bqkv)
    Q, K, V = qkv[..., :E], qkv[..., E:2 * E], qkv[..., 2 * E:]
    emb = sinu_pos_emb(E, S)
    c, s = np.cos(emb), np.sin(emb)
    Q = Q * c + rotate_half(Q) * s
    K = K * c - rotate_half(K) * s
    return Q, K, V

@@ -1,0 +1,284 @@
+import math
+from contextlib import ExitStack
+
+import concourse.mybir as mybir
+from concourse.masks import make_identity
+
+F32 = mybir.dt.float32
+BF16 = mybir.dt.bfloat16
+U32 = mybir.dt.uint32
+U8 = mybir.dt.uint8
+FP8X4 = mybir.dt.float8_e4m3fn_x4
+ALU = mybir.AluOpType
+ACT = mybir.ActivationFunctionType
+
+P = 128
+TOKENS = 256
+POSITIONS = 64
+TOKEN_TILES = TOKENS // P
+D = 2048
+E = 2048
+HALF_E = E // 2
+EPS = 1e-5
+
+PACK = 4
+K_PASS = P * PACK
+PASSES = D // K_PASS
+WORDS_PER_PASS = K_PASS // 2
+
+CHUNK = 512
+ROW_TILES = CHUNK // P
+CHUNKS = 3 * E // CHUNK
+CHUNKS_PER_OUTPUT = E // CHUNK
+SLAB_PASSES = 2
+SLABS_PER_CHUNK = PASSES // SLAB_PASSES
+SLABS = CHUNKS * SLABS_PER_CHUNK
+SLABS_AHEAD = 4
+SLABS_BEFORE_X = 2
+W_BUFS = 4
+
+ROUND = 1.5 * 2.0**23
+FREQ_RATIO = 10000.0 ** (-1.0 / HALF_E)
+REDUCED = HALF_E // 2
+
+FLOPS = 2 * TOKENS * D * 3 * E
+
+
+def tile_rotaryembeddingtransformerlayer_pa_kernel(
+    tc, src, Wqkv, bqkv, g1, be1, out_q, out_k, out_v
+):
+    nc = tc.nc
+    x_rows = src.flatten_outer_dims()
+    out_rows = [out_q.flatten_outer_dims(), out_k.flatten_outer_dims(), out_v.flatten_outer_dims()]
+
+    with ExitStack() as pools:
+        pools.enter_context(tc.manual_schedule())
+        const = pools.enter_context(tc.tile_pool(name="const", bufs=1))
+        w_pool = pools.enter_context(tc.tile_pool(name="w_raw", bufs=W_BUFS))
+        grouped_pool = pools.enter_context(tc.tile_pool(name="grouped", bufs=SLABS_AHEAD))
+        code_pool = pools.enter_context(tc.tile_pool(name="codes", bufs=SLABS_AHEAD + 2))
+        psum_tr = pools.enter_context(tc.psum_pool(name="psum_tr", bufs=4))
+        psum_acc = pools.enter_context(tc.psum_pool(name="psum_acc", bufs=4))
+
+        ident = const.tile([P, P], F32)
+        bias_bc = const.tile([P, 3 * E], BF16)
+        x_codes = const.tile([P, PASSES * TOKENS], U32, align_bytes=64)
+        x_scales = const.tile([P, PASSES * TOKENS], U8, align_bytes=64)
+        cos_t = const.tile([P, E], F32)
+        sin_t = const.tile([P, E], F32)
+
+        w_raw = {}
+        w_codes = {}
+        w_scales = {}
+        acc = {}
+        q_rows = {}
+        mixed = {}
+
+        def load_chunk(c):
+            w_raw[c] = w_pool.tile([P, ROW_TILES, D], BF16, name="w_raw")
+            nc.sync.dma_start(
+                out=w_raw[c][:],
+                in_=Wqkv[c * CHUNK : (c + 1) * CHUNK, :].rearrange("(p t) k -> p t k", t=ROW_TILES),
+            )
+            if c % CHUNKS_PER_OUTPUT == 0:
+                span = slice(c * CHUNK, c * CHUNK + E)
+                nc.sync.dma_start(out=bias_bc[:, span], in_=bqkv[span].partition_broadcast(P))
+
+        def transpose_words(rows_of, g, width, dest_words):
+            w_t = psum_tr.tile([P, 2, width], F32, name="w_t", tag="tr")
+            for j in range(width // P):
+                words = rows_of(j).bitcast(F32)
+                for u in range(2):
+                    pair = slice(g * WORDS_PER_PASS + u, (g + 1) * WORDS_PER_PASS, 2)
+                    nc.tensor.transpose(w_t[:, u, j * P : (j + 1) * P], words[:, pair], ident[:])
+            nc.scalar.copy(out=dest_words, in_=w_t[:].rearrange("p u n -> p n u"))
+
+        def prepare(slab):
+            c, part = divmod(slab, SLABS_PER_CHUNK)
+            grouped = grouped_pool.tile(
+                [P, SLAB_PASSES * CHUNK * PACK], BF16, name="grouped", align_bytes=64
+            )
+            grouped_words = grouped[:].bitcast(F32).rearrange("p (i n u) -> p i n u", i=SLAB_PASSES, u=2)
+            for i in range(SLAB_PASSES):
+                for h in range(2):
+                    transpose_words(
+                        lambda j: w_raw[c][:, 2 * h + j, :],
+                        part * SLAB_PASSES + i,
+                        2 * P,
+                        grouped_words[:, i, h * 2 * P : (h + 1) * 2 * P, :],
+                    )
+            w_codes[slab] = code_pool.tile([P, SLAB_PASSES * CHUNK], U32, name="w_codes", align_bytes=64)
+            w_scales[slab] = code_pool.tile([P, SLAB_PASSES * CHUNK], U8, name="w_scales", align_bytes=64)
+            nc.vector.quantize_mx(
+                out=w_codes[slab][:].bitcast(FP8X4), scales=w_scales[slab][:], in_=grouped[:]
+            )
+            if part == SLABS_PER_CHUNK - 1 and c + W_BUFS < CHUNKS:
+                load_chunk(c + W_BUFS)
+
+        with tc.tile_pool(name="head", bufs=1) as head:
+            x_raw = []
+            for m in range(TOKEN_TILES):
+                x_raw.append(head.tile([P, D], BF16, name="x_raw%d" % m))
+                nc.sync.dma_start(out=x_raw[m][:], in_=x_rows[m * P : (m + 1) * P, :])
+            gain_bc = head.tile([P, D], BF16)
+            nc.sync.dma_start(out=gain_bc[:], in_=g1.partition_broadcast(P))
+            shift_bc = head.tile([P, D], BF16)
+            nc.sync.dma_start(out=shift_bc[:], in_=be1.partition_broadcast(P))
+            for c in range(W_BUFS):
+                load_chunk(c)
+
+            pos = head.tile([P, 1], F32)
+            for first in range(0, P, POSITIONS):
+                nc.gpsimd.iota(
+                    pos[first : first + POSITIONS, :],
+                    pattern=[[0, 1]],
+                    base=0,
+                    channel_multiplier=1,
+                    allow_small_or_imprecise_dtypes=True,
+                )
+            turns = head.tile([P, HALF_E], F32)
+            nc.gpsimd.tensor_scalar(
+                out=turns[:, 0:1], in0=pos[:], scalar1=1.0 / (2.0 * math.pi), scalar2=0.0,
+                op0=ALU.mult, op1=ALU.add,
+            )
+            make_identity(nc, ident[:])
+            n = 1
+            while n < HALF_E:
+                nc.vector.tensor_scalar(
+                    out=turns[:, n : 2 * n], in0=turns[:, 0:n], scalar1=FREQ_RATIO**n, scalar2=None,
+                    op0=ALU.mult,
+                )
+                n *= 2
+            whole = head.tile([P, REDUCED], F32)
+            nc.vector.tensor_scalar(
+                out=whole[:], in0=turns[:, 0:REDUCED], scalar1=ROUND, scalar2=ROUND,
+                op0=ALU.add, op1=ALU.subtract,
+            )
+            nc.vector.tensor_tensor(
+                out=turns[:, 0:REDUCED], in0=turns[:, 0:REDUCED], in1=whole[:], op=ALU.subtract
+            )
+            abs_turns = head.tile([P, HALF_E], F32)
+            nc.vector.scalar_tensor_tensor(
+                out=abs_turns[:], in0=turns[:], scalar=-1.0, in1=turns[:], op0=ALU.mult, op1=ALU.max
+            )
+            nc.scalar.activation(out=cos_t[:, 0:HALF_E], in_=turns[:], func=ACT.Sin, scale=2.0 * math.pi)
+            nc.scalar.activation(
+                out=cos_t[:, HALF_E:E], in_=abs_turns[:], func=ACT.Sin,
+                scale=-2.0 * math.pi, bias=math.pi / 2.0,
+            )
+            nc.scalar.activation(out=sin_t[:, 0:HALF_E], in_=cos_t[:, 0:HALF_E], func=ACT.Sin, scale=-1.0)
+            nc.scalar.activation(out=sin_t[:, HALF_E:E], in_=cos_t[:, HALF_E:E], func=ACT.Sin)
+            nc.scalar.activation(out=cos_t[:], in_=cos_t[:], func=ACT.Sin, bias=math.pi / 2.0)
+
+            mean_var = head.tile([P, TOKEN_TILES, 2], F32)
+            for m in range(TOKEN_TILES):
+                stats = head.tile([P, D // 512, 6], F32, name="stats%d" % m)
+                for j in range(D // 512):
+                    nc.vector.bn_stats(out=stats[:, j, :], in_=x_raw[m][:, j * 512 : (j + 1) * 512])
+                nc.vector.bn_aggr(out=mean_var[:, m, :], in_=stats[:].rearrange("p c s -> p (c s)"))
+            std = head.tile([P, TOKEN_TILES], F32)
+            nc.scalar.activation(out=std[:], in_=mean_var[:, :, 1], func=ACT.Sqrt, bias=EPS)
+            centred = []
+            for m in range(TOKEN_TILES):
+                centred.append(head.tile([P, D], F32, name="centred%d" % m))
+                nc.vector.scalar_tensor_tensor(
+                    out=centred[m][:], in0=x_raw[m][:], scalar=mean_var[:, m, 0:1], in1=gain_bc[:],
+                    op0=ALU.subtract, op1=ALU.mult,
+                )
+            rstd = head.tile([P, TOKEN_TILES], F32)
+            nc.vector.reciprocal(out=rstd[:], in_=std[:])
+            xn = []
+            for m in range(TOKEN_TILES):
+                xn.append(head.tile([P, D], BF16, name="xn%d" % m))
+                nc.vector.scalar_tensor_tensor(
+                    out=xn[m][:], in0=centred[m][:], scalar=rstd[:, m : m + 1], in1=shift_bc[:],
+                    op0=ALU.mult, op1=ALU.add,
+                )
+
+            for slab in range(SLABS_BEFORE_X):
+                prepare(slab)
+
+            grouped_x = head.tile([P, PASSES * TOKENS * PACK], BF16, align_bytes=64)
+            grouped_x_words = grouped_x[:].bitcast(F32).rearrange("p (g r u) -> p g r u", g=PASSES, u=2)
+            for g in range(PASSES):
+                transpose_words(lambda m: xn[m][:], g, TOKENS, grouped_x_words[:, g, :, :])
+            nc.vector.quantize_mx(out=x_codes[:].bitcast(FP8X4), scales=x_scales[:], in_=grouped_x[:])
+
+            for slab in range(SLABS_BEFORE_X, SLABS_AHEAD):
+                prepare(slab)
+
+        rot = pools.enter_context(tc.tile_pool(name="rot", bufs=4))
+
+        def add_bias(c, m, dest):
+            nc.vector.tensor_tensor(
+                out=dest.rearrange("r (p t) -> r p t", t=ROW_TILES),
+                in0=acc[m][:].rearrange("r (t p) -> r p t", t=ROW_TILES),
+                in1=bias_bc[:, c * CHUNK : (c + 1) * CHUNK].rearrange("r (p t) -> r p t", t=ROW_TILES),
+                op=ALU.add,
+            )
+
+        def finish_v(c):
+            cc = c % CHUNKS_PER_OUTPUT
+            for m in range(TOKEN_TILES):
+                v_rows = rot.tile([P, CHUNK], F32, name="v_rows")
+                add_bias(c, m, v_rows[:])
+                nc.sync.dma_start(
+                    out=out_rows[2][m * P : (m + 1) * P, cc * CHUNK : (cc + 1) * CHUNK], in_=v_rows[:]
+                )
+
+        def finish_q_or_k(c):
+            which, cc = divmod(c, CHUNKS_PER_OUTPUT)
+            for m in range(TOKEN_TILES):
+                if cc == 0:
+                    q_rows[m] = rot.tile([P, E], F32, name="q_rows")
+                    mixed[m] = rot.tile([P, E], F32, name="mixed", bufs=TOKEN_TILES)
+                add_bias(c, m, q_rows[m][:, cc * CHUNK : (cc + 1) * CHUNK])
+            if cc % 2 == 1:
+                j = cc // 2
+                span = slice(j * HALF_E, (j + 1) * HALF_E)
+                for m in range(TOKEN_TILES):
+                    nc.vector.tensor_tensor(
+                        out=mixed[m][:].rearrange("r (h j i) -> r h j i", h=2, j=2)[:, :, j, :],
+                        in0=q_rows[m][:, span].rearrange("r (i h) -> r h i", h=2),
+                        in1=sin_t[:].rearrange("r (h j i) -> r h j i", h=2, j=2)[:, :, j, :],
+                        op=ALU.mult,
+                    )
+                for m in range(TOKEN_TILES):
+                    nc.vector.tensor_tensor(
+                        out=q_rows[m][:, span], in0=q_rows[m][:, span], in1=cos_t[:, span], op=ALU.mult
+                    )
+            if cc == CHUNKS_PER_OUTPUT - 1:
+                for m in range(TOKEN_TILES):
+                    nc.vector.tensor_tensor(
+                        out=q_rows[m][:], in0=q_rows[m][:], in1=mixed[m][:],
+                        op=(ALU.add if which == 0 else ALU.subtract),
+                    )
+                    nc.gpsimd.dma_start(out=out_rows[which][m * P : (m + 1) * P, :], in_=q_rows[m][:])
+
+        def multiply(slab):
+            c, part = divmod(slab, SLABS_PER_CHUNK)
+            for i in range(SLAB_PASSES):
+                g = part * SLAB_PASSES + i
+                for m in range(TOKEN_TILES):
+                    if g == 0:
+                        acc[m] = psum_acc.tile([P, CHUNK], F32, name="acc", tag="acc")
+                    tokens = slice(g * TOKENS + m * P, g * TOKENS + (m + 1) * P)
+                    nc.tensor.matmul_mx(
+                        out=acc[m][:],
+                        lhsT=x_codes[:, tokens].bitcast(FP8X4),
+                        lhsT_scale=x_scales[:, tokens],
+                        rhs=w_codes[slab][:, i * CHUNK : (i + 1) * CHUNK].bitcast(FP8X4),
+                        rhs_scale=w_scales[slab][:, i * CHUNK : (i + 1) * CHUNK],
+                        start=(g == 0),
+                        stop=(g == PASSES - 1),
+                    )
+            if part == SLABS_PER_CHUNK - 1:
+                if c < 2 * CHUNKS_PER_OUTPUT:
+                    finish_q_or_k(c)
+                else:
+                    finish_v(c)
+
+        for slab in range(SLABS_AHEAD, SLABS + SLABS_AHEAD):
+            multiply(slab - SLABS_AHEAD)
+            if slab < SLABS:
+                prepare(slab)

@@ -31,11 +31,14 @@ ROW_TILES = CHUNK // P
 CHUNKS = 3 * E // CHUNK
 CHUNKS_PER_OUTPUT = E // CHUNK
 SLAB_PASSES = 2
+SLAB_K = SLAB_PASSES * K_PASS
 SLABS_PER_CHUNK = PASSES // SLAB_PASSES
 SLABS = CHUNKS * SLABS_PER_CHUNK
-SLABS_AHEAD = 4
-SLABS_BEFORE_X = 2
-W_BUFS = 4
+SLABS_PER_OUTPUT = CHUNKS_PER_OUTPUT * SLABS_PER_CHUNK
+SLABS_AHEAD = 9
+W_BUFS = 6
+GROUPED_BUFS = 4
+CODE_BUFS = SLABS_AHEAD + 2
 
 ROUND = 1.5 * 2.0**23
 FREQ_RATIO = 10000.0 ** (-1.0 / HALF_E)
@@ -55,8 +58,8 @@ def tile_rotaryembeddingtransformerlayer_pa_kernel(
         pools.enter_context(tc.manual_schedule())
         const = pools.enter_context(tc.tile_pool(name="const", bufs=1))
         w_pool = pools.enter_context(tc.tile_pool(name="w_raw", bufs=W_BUFS))
-        grouped_pool = pools.enter_context(tc.tile_pool(name="grouped", bufs=SLABS_AHEAD))
-        code_pool = pools.enter_context(tc.tile_pool(name="codes", bufs=SLABS_AHEAD + 2))
+        grouped_pool = pools.enter_context(tc.tile_pool(name="grouped", bufs=GROUPED_BUFS))
+        code_pool = pools.enter_context(tc.tile_pool(name="codes", bufs=CODE_BUFS))
         psum_tr = pools.enter_context(tc.psum_pool(name="psum_tr", bufs=4))
         psum_acc = pools.enter_context(tc.psum_pool(name="psum_acc", bufs=4))
 
@@ -68,65 +71,76 @@ def tile_rotaryembeddingtransformerlayer_pa_kernel(
         sin_t = const.tile([P, E], F32)
 
         w_raw = {}
+        grouped = {}
         w_codes = {}
         w_scales = {}
         acc = {}
         q_rows = {}
         mixed = {}
 
-        def load_chunk(c):
-            w_raw[c] = w_pool.tile([P, ROW_TILES, D], BF16, name="w_raw")
+        def load_slab(slab):
+            c, part = divmod(slab, SLABS_PER_CHUNK)
+            w_raw[slab] = w_pool.tile([P, ROW_TILES, SLAB_K], BF16, name="w_raw")
             nc.sync.dma_start(
-                out=w_raw[c][:],
-                in_=Wqkv[c * CHUNK : (c + 1) * CHUNK, :].rearrange("(p t) k -> p t k", t=ROW_TILES),
+                out=w_raw[slab][:],
+                in_=Wqkv[c * CHUNK : (c + 1) * CHUNK, part * SLAB_K : (part + 1) * SLAB_K].rearrange(
+                    "(p t) k -> p t k", t=ROW_TILES
+                ),
             )
-            if c % CHUNKS_PER_OUTPUT == 0:
-                span = slice(c * CHUNK, c * CHUNK + E)
+            which, rest = divmod(slab, SLABS_PER_OUTPUT)
+            if rest == 2:
+                span = slice(which * E, (which + 1) * E)
                 nc.sync.dma_start(out=bias_bc[:, span], in_=bqkv[span].partition_broadcast(P))
 
-        def transpose_words(rows_of, g, width, dest_words):
+        def transpose_words(rows_of, w0, width, dest_words):
             w_t = psum_tr.tile([P, 2, width], F32, name="w_t", tag="tr")
             for j in range(width // P):
                 words = rows_of(j).bitcast(F32)
                 for u in range(2):
-                    pair = slice(g * WORDS_PER_PASS + u, (g + 1) * WORDS_PER_PASS, 2)
+                    pair = slice(w0 + u, w0 + WORDS_PER_PASS, 2)
                     nc.tensor.transpose(w_t[:, u, j * P : (j + 1) * P], words[:, pair], ident[:])
             nc.scalar.copy(out=dest_words, in_=w_t[:].rearrange("p u n -> p n u"))
 
-        def prepare(slab):
-            c, part = divmod(slab, SLABS_PER_CHUNK)
-            grouped = grouped_pool.tile(
+        def transpose_slab(slab):
+            grouped[slab] = grouped_pool.tile(
                 [P, SLAB_PASSES * CHUNK * PACK], BF16, name="grouped", align_bytes=64
             )
-            grouped_words = grouped[:].bitcast(F32).rearrange("p (i n u) -> p i n u", i=SLAB_PASSES, u=2)
+            words = grouped[slab][:].bitcast(F32).rearrange("p (i n u) -> p i n u", i=SLAB_PASSES, u=2)
             for i in range(SLAB_PASSES):
                 for h in range(2):
                     transpose_words(
-                        lambda j: w_raw[c][:, 2 * h + j, :],
-                        part * SLAB_PASSES + i,
+                        lambda j: w_raw[slab][:, 2 * h + j, :],
+                        i * WORDS_PER_PASS,
                         2 * P,
-                        grouped_words[:, i, h * 2 * P : (h + 1) * 2 * P, :],
+                        words[:, i, h * 2 * P : (h + 1) * 2 * P, :],
                     )
+            if slab + W_BUFS < SLABS:
+                load_slab(slab + W_BUFS)
+
+        def quantise_slab(slab):
             w_codes[slab] = code_pool.tile([P, SLAB_PASSES * CHUNK], U32, name="w_codes", align_bytes=64)
             w_scales[slab] = code_pool.tile([P, SLAB_PASSES * CHUNK], U8, name="w_scales", align_bytes=64)
             nc.vector.quantize_mx(
-                out=w_codes[slab][:].bitcast(FP8X4), scales=w_scales[slab][:], in_=grouped[:]
+                out=w_codes[slab][:].bitcast(FP8X4), scales=w_scales[slab][:], in_=grouped[slab][:]
             )
-            if part == SLABS_PER_CHUNK - 1 and c + W_BUFS < CHUNKS:
-                load_chunk(c + W_BUFS)
 
         with tc.tile_pool(name="head", bufs=1) as head:
             x_raw = []
             for m in range(TOKEN_TILES):
                 x_raw.append(head.tile([P, D], BF16, name="x_raw%d" % m))
                 nc.sync.dma_start(out=x_raw[m][:], in_=x_rows[m * P : (m + 1) * P, :])
+            load_slab(0)
             gain_bc = head.tile([P, D], BF16)
             nc.sync.dma_start(out=gain_bc[:], in_=g1.partition_broadcast(P))
+            load_slab(1)
             shift_bc = head.tile([P, D], BF16)
             nc.sync.dma_start(out=shift_bc[:], in_=be1.partition_broadcast(P))
-            for c in range(W_BUFS):
-                load_chunk(c)
+            for slab in range(2, W_BUFS):
+                load_slab(slab)
 
+            turns = sin_t[:, 0:HALF_E]
+            abs_turns = sin_t[:, HALF_E : HALF_E + REDUCED]
+            whole = sin_t[:, HALF_E + REDUCED : E]
             pos = head.tile([P, 1], F32)
             for first in range(0, P, POSITIONS):
                 nc.gpsimd.iota(
@@ -136,12 +150,13 @@ def tile_rotaryembeddingtransformerlayer_pa_kernel(
                     channel_multiplier=1,
                     allow_small_or_imprecise_dtypes=True,
                 )
-            turns = head.tile([P, HALF_E], F32)
             nc.gpsimd.tensor_scalar(
                 out=turns[:, 0:1], in0=pos[:], scalar1=1.0 / (2.0 * math.pi), scalar2=0.0,
                 op0=ALU.mult, op1=ALU.add,
             )
             make_identity(nc, ident[:])
+            minus_half = head.tile([P, 1], F32)
+            nc.gpsimd.memset(minus_half[:], -0.5)
             n = 1
             while n < HALF_E:
                 nc.vector.tensor_scalar(
@@ -149,26 +164,30 @@ def tile_rotaryembeddingtransformerlayer_pa_kernel(
                     op0=ALU.mult,
                 )
                 n *= 2
-            whole = head.tile([P, REDUCED], F32)
+            low, high = slice(0, REDUCED), slice(REDUCED, HALF_E)
             nc.vector.tensor_scalar(
-                out=whole[:], in0=turns[:, 0:REDUCED], scalar1=ROUND, scalar2=ROUND,
-                op0=ALU.add, op1=ALU.subtract,
+                out=whole, in0=turns[:, low], scalar1=ROUND, scalar2=ROUND, op0=ALU.add, op1=ALU.subtract
             )
-            nc.vector.tensor_tensor(
-                out=turns[:, 0:REDUCED], in0=turns[:, 0:REDUCED], in1=whole[:], op=ALU.subtract
-            )
-            abs_turns = head.tile([P, HALF_E], F32)
+            nc.vector.tensor_tensor(out=turns[:, low], in0=turns[:, low], in1=whole, op=ALU.subtract)
             nc.vector.scalar_tensor_tensor(
-                out=abs_turns[:], in0=turns[:], scalar=-1.0, in1=turns[:], op0=ALU.mult, op1=ALU.max
+                out=abs_turns, in0=turns[:, low], scalar=-1.0, in1=turns[:, low], op0=ALU.mult, op1=ALU.max
             )
-            nc.scalar.activation(out=cos_t[:, 0:HALF_E], in_=turns[:], func=ACT.Sin, scale=2.0 * math.pi)
-            nc.scalar.activation(
-                out=cos_t[:, HALF_E:E], in_=abs_turns[:], func=ACT.Sin,
-                scale=-2.0 * math.pi, bias=math.pi / 2.0,
-            )
+            for span, magnitudes in ((high, turns[:, high]), (low, abs_turns)):
+                nc.scalar.activation(
+                    out=cos_t[:, span], in_=turns[:, span], func=ACT.Sin, scale=2.0 * math.pi
+                )
+                nc.scalar.activation(
+                    out=cos_t[:, HALF_E + span.start : HALF_E + span.stop], in_=magnitudes, func=ACT.Sin,
+                    scale=-2.0 * math.pi, bias=math.pi / 2.0,
+                )
+
+            transpose_slab(0)
             nc.scalar.activation(out=sin_t[:, 0:HALF_E], in_=cos_t[:, 0:HALF_E], func=ACT.Sin, scale=-1.0)
             nc.scalar.activation(out=sin_t[:, HALF_E:E], in_=cos_t[:, HALF_E:E], func=ACT.Sin)
+            transpose_slab(1)
             nc.scalar.activation(out=cos_t[:], in_=cos_t[:], func=ACT.Sin, bias=math.pi / 2.0)
+            transpose_slab(2)
+            transpose_slab(3)
 
             mean_var = head.tile([P, TOKEN_TILES, 2], F32)
             for m in range(TOKEN_TILES):
@@ -176,36 +195,45 @@ def tile_rotaryembeddingtransformerlayer_pa_kernel(
                 for j in range(D // 512):
                     nc.vector.bn_stats(out=stats[:, j, :], in_=x_raw[m][:, j * 512 : (j + 1) * 512])
                 nc.vector.bn_aggr(out=mean_var[:, m, :], in_=stats[:].rearrange("p c s -> p (c s)"))
-            std = head.tile([P, TOKEN_TILES], F32)
-            nc.scalar.activation(out=std[:], in_=mean_var[:, :, 1], func=ACT.Sqrt, bias=EPS)
+            rstd = []
+            for m in range(TOKEN_TILES):
+                rstd.append(head.tile([P, 1], F32, name="rstd%d" % m))
+                nc.gpsimd.tensor_scalar(
+                    out=rstd[m][:], in0=mean_var[:, m, 1:2], scalar1=1.0, scalar2=EPS,
+                    op0=ALU.mult, op1=ALU.add,
+                )
+                nc.gpsimd.tensor_tensor(out=rstd[m][:], in0=rstd[m][:], in1=minus_half[:], op=ALU.pow)
             centred = []
+            xn = []
             for m in range(TOKEN_TILES):
                 centred.append(head.tile([P, D], F32, name="centred%d" % m))
                 nc.vector.scalar_tensor_tensor(
                     out=centred[m][:], in0=x_raw[m][:], scalar=mean_var[:, m, 0:1], in1=gain_bc[:],
                     op0=ALU.subtract, op1=ALU.mult,
                 )
-            rstd = head.tile([P, TOKEN_TILES], F32)
-            nc.vector.reciprocal(out=rstd[:], in_=std[:])
-            xn = []
+                quantise_slab(m)
+            transpose_slab(4)
             for m in range(TOKEN_TILES):
                 xn.append(head.tile([P, D], BF16, name="xn%d" % m))
                 nc.vector.scalar_tensor_tensor(
-                    out=xn[m][:], in0=centred[m][:], scalar=rstd[:, m : m + 1], in1=shift_bc[:],
+                    out=xn[m][:], in0=centred[m][:], scalar=rstd[m][:], in1=shift_bc[:],
                     op0=ALU.mult, op1=ALU.add,
                 )
-
-            for slab in range(SLABS_BEFORE_X):
-                prepare(slab)
+                quantise_slab(TOKEN_TILES + m)
+            transpose_slab(5)
 
             grouped_x = head.tile([P, PASSES * TOKENS * PACK], BF16, align_bytes=64)
             grouped_x_words = grouped_x[:].bitcast(F32).rearrange("p (g r u) -> p g r u", g=PASSES, u=2)
             for g in range(PASSES):
-                transpose_words(lambda m: xn[m][:], g, TOKENS, grouped_x_words[:, g, :, :])
+                transpose_words(lambda m: xn[m][:], g * WORDS_PER_PASS, TOKENS, grouped_x_words[:, g, :, :])
+            quantise_slab(4)
             nc.vector.quantize_mx(out=x_codes[:].bitcast(FP8X4), scales=x_scales[:], in_=grouped_x[:])
+            quantise_slab(5)
 
-            for slab in range(SLABS_BEFORE_X, SLABS_AHEAD):
-                prepare(slab)
+        for slab in range(6, SLABS_AHEAD):
+            transpose_slab(slab)
+            if slab > 6:
+                quantise_slab(slab - 1)
 
         rot = pools.enter_context(tc.tile_pool(name="rot", bufs=4))
 
@@ -272,13 +300,16 @@ def tile_rotaryembeddingtransformerlayer_pa_kernel(
                         start=(g == 0),
                         stop=(g == PASSES - 1),
                     )
+
+        for slab in range(SLABS_AHEAD, SLABS + SLABS_AHEAD):
+            multiply(slab - SLABS_AHEAD)
+            if slab < SLABS:
+                transpose_slab(slab)
+            if slab <= SLABS:
+                quantise_slab(slab - 1)
+            c, part = divmod(slab - SLABS_AHEAD, SLABS_PER_CHUNK)
             if part == SLABS_PER_CHUNK - 1:
                 if c < 2 * CHUNKS_PER_OUTPUT:
                     finish_q_or_k(c)
                 else:
                     finish_v(c)
-
-        for slab in range(SLABS_AHEAD, SLABS + SLABS_AHEAD):
-            multiply(slab - SLABS_AHEAD)
-            if slab < SLABS:
-                prepare(slab)

@@ -30,13 +30,23 @@ CHUNK = 512
 ROW_TILES = CHUNK // P
 CHUNKS = 3 * E // CHUNK
 CHUNKS_PER_OUTPUT = E // CHUNK
+FIRST_Q, FIRST_K, FIRST_V = 0, CHUNKS_PER_OUTPUT, 2 * CHUNKS_PER_OUTPUT
+ORDER = (
+    [FIRST_V]
+    + list(range(FIRST_Q, FIRST_K))
+    + [FIRST_V + 1]
+    + list(range(FIRST_K, FIRST_V))
+    + [FIRST_V + 2, FIRST_V + 3]
+)
 SLAB_PASSES = 2
 SLAB_K = SLAB_PASSES * K_PASS
+SLAB_WORDS = SLAB_K // 2
 SLABS_PER_CHUNK = PASSES // SLAB_PASSES
 SLABS = CHUNKS * SLABS_PER_CHUNK
-SLABS_PER_OUTPUT = CHUNKS_PER_OUTPUT * SLABS_PER_CHUNK
-SLABS_AHEAD = 9
-W_BUFS = 6
+SLABS_AHEAD = 3
+SLABS_BEFORE_X = 2
+W_BUFS = 5
+MIX_STEPS = 2
 GROUPED_BUFS = 4
 CODE_BUFS = SLABS_AHEAD + 2
 
@@ -77,45 +87,46 @@ def tile_rotaryembeddingtransformerlayer_pa_kernel(
         acc = {}
         q_rows = {}
         mixed = {}
+        mix_queue = []
 
-        def load_slab(slab):
-            c, part = divmod(slab, SLABS_PER_CHUNK)
-            w_raw[slab] = w_pool.tile([P, ROW_TILES, SLAB_K], BF16, name="w_raw")
-            nc.sync.dma_start(
-                out=w_raw[slab][:],
-                in_=Wqkv[c * CHUNK : (c + 1) * CHUNK, part * SLAB_K : (part + 1) * SLAB_K].rearrange(
-                    "(p t) k -> p t k", t=ROW_TILES
-                ),
-            )
-            which, rest = divmod(slab, SLABS_PER_OUTPUT)
-            if rest == 2:
-                span = slice(which * E, (which + 1) * E)
+        def load_chunk(i, parts):
+            c = ORDER[i]
+            w_raw[i] = w_pool.tile([P, ROW_TILES, D], BF16, name="w_raw")
+            for part in range(parts):
+                k = slice(part * (D // parts), (part + 1) * (D // parts))
+                nc.sync.dma_start(
+                    out=w_raw[i][:, :, k],
+                    in_=Wqkv[c * CHUNK : (c + 1) * CHUNK, k].rearrange("(p t) k -> p t k", t=ROW_TILES),
+                )
+                if i == 0 and part == 0:
+                    nc.sync.dma_start(out=shift_bc[:], in_=be1.partition_broadcast(P))
+            if c in (FIRST_Q, FIRST_K, FIRST_V):
+                span = slice(c * CHUNK, c * CHUNK + E)
                 nc.sync.dma_start(out=bias_bc[:, span], in_=bqkv[span].partition_broadcast(P))
 
-        def transpose_words(rows_of, w0, width, dest_words):
+        def transpose_words(words_of, width, dest_words):
             w_t = psum_tr.tile([P, 2, width], F32, name="w_t", tag="tr")
             for j in range(width // P):
-                words = rows_of(j).bitcast(F32)
                 for u in range(2):
-                    pair = slice(w0 + u, w0 + WORDS_PER_PASS, 2)
-                    nc.tensor.transpose(w_t[:, u, j * P : (j + 1) * P], words[:, pair], ident[:])
+                    nc.tensor.transpose(w_t[:, u, j * P : (j + 1) * P], words_of(j, u), ident[:])
             nc.scalar.copy(out=dest_words, in_=w_t[:].rearrange("p u n -> p n u"))
 
         def transpose_slab(slab):
+            i, part = divmod(slab, SLABS_PER_CHUNK)
             grouped[slab] = grouped_pool.tile(
                 [P, SLAB_PASSES * CHUNK * PACK], BF16, name="grouped", align_bytes=64
             )
-            words = grouped[slab][:].bitcast(F32).rearrange("p (i n u) -> p i n u", i=SLAB_PASSES, u=2)
-            for i in range(SLAB_PASSES):
+            dest = grouped[slab][:].bitcast(F32).rearrange("p (g n u) -> p g n u", g=SLAB_PASSES, u=2)
+            for g in range(SLAB_PASSES):
+                w0 = part * SLAB_WORDS + g * WORDS_PER_PASS
                 for h in range(2):
                     transpose_words(
-                        lambda j: w_raw[slab][:, 2 * h + j, :],
-                        i * WORDS_PER_PASS,
+                        lambda j, u: w_raw[i][:, 2 * h + j, :].bitcast(F32)[:, w0 + u : w0 + WORDS_PER_PASS : 2],
                         2 * P,
-                        words[:, i, h * 2 * P : (h + 1) * 2 * P, :],
+                        dest[:, g, h * 2 * P : (h + 1) * 2 * P, :],
                     )
-            if slab + W_BUFS < SLABS:
-                load_slab(slab + W_BUFS)
+            if part == SLABS_PER_CHUNK - 1 and i + W_BUFS < CHUNKS:
+                load_chunk(i + W_BUFS, 1)
 
         def quantise_slab(slab):
             w_codes[slab] = code_pool.tile([P, SLAB_PASSES * CHUNK], U32, name="w_codes", align_bytes=64)
@@ -124,23 +135,54 @@ def tile_rotaryembeddingtransformerlayer_pa_kernel(
                 out=w_codes[slab][:].bitcast(FP8X4), scales=w_scales[slab][:], in_=grouped[slab][:]
             )
 
+        turns = sin_t[:, 0:HALF_E]
+        abs_turns = sin_t[:, HALF_E : HALF_E + REDUCED]
+        whole = sin_t[:, HALF_E + REDUCED : E]
+
+        def double_turns(first, last):
+            n = first
+            while n < last:
+                nc.vector.tensor_scalar(
+                    out=turns[:, n : 2 * n], in0=turns[:, 0:n], scalar1=FREQ_RATIO**n, scalar2=None,
+                    op0=ALU.mult,
+                )
+                n *= 2
+
+        def reduce_turns():
+            low = turns[:, 0:REDUCED]
+            nc.vector.tensor_scalar(
+                out=whole, in0=low, scalar1=ROUND, scalar2=ROUND, op0=ALU.add, op1=ALU.subtract
+            )
+            nc.vector.tensor_tensor(out=low, in0=low, in1=whole, op=ALU.subtract)
+
+        def fill_emb():
+            nc.scalar.activation(out=cos_t[:, 0:HALF_E], in_=turns, func=ACT.Sin, scale=2.0 * math.pi)
+            nc.scalar.activation(out=abs_turns, in_=turns[:, 0:REDUCED], func=ACT.Abs)
+            for first, magnitudes in ((0, abs_turns), (REDUCED, turns[:, REDUCED:HALF_E])):
+                nc.scalar.activation(
+                    out=cos_t[:, HALF_E + first : HALF_E + first + REDUCED], in_=magnitudes, func=ACT.Sin,
+                    scale=-2.0 * math.pi, bias=math.pi / 2.0,
+                )
+
+        def fill_sin():
+            nc.scalar.activation(out=sin_t[:, 0:HALF_E], in_=cos_t[:, 0:HALF_E], func=ACT.Sin, scale=-1.0)
+            nc.scalar.activation(out=sin_t[:, HALF_E:E], in_=cos_t[:, HALF_E:E], func=ACT.Sin)
+
+        def fill_cos():
+            nc.scalar.activation(out=cos_t[:], in_=cos_t[:], func=ACT.Sin, bias=math.pi / 2.0)
+
         with tc.tile_pool(name="head", bufs=1) as head:
             x_raw = []
             for m in range(TOKEN_TILES):
                 x_raw.append(head.tile([P, D], BF16, name="x_raw%d" % m))
                 nc.sync.dma_start(out=x_raw[m][:], in_=x_rows[m * P : (m + 1) * P, :])
-            load_slab(0)
             gain_bc = head.tile([P, D], BF16)
             nc.sync.dma_start(out=gain_bc[:], in_=g1.partition_broadcast(P))
-            load_slab(1)
             shift_bc = head.tile([P, D], BF16)
-            nc.sync.dma_start(out=shift_bc[:], in_=be1.partition_broadcast(P))
-            for slab in range(2, W_BUFS):
-                load_slab(slab)
+            load_chunk(0, SLABS_PER_CHUNK)
+            for i in range(1, W_BUFS):
+                load_chunk(i, 1)
 
-            turns = sin_t[:, 0:HALF_E]
-            abs_turns = sin_t[:, HALF_E : HALF_E + REDUCED]
-            whole = sin_t[:, HALF_E + REDUCED : E]
             pos = head.tile([P, 1], F32)
             for first in range(0, P, POSITIONS):
                 nc.gpsimd.iota(
@@ -157,83 +199,72 @@ def tile_rotaryembeddingtransformerlayer_pa_kernel(
             make_identity(nc, ident[:])
             minus_half = head.tile([P, 1], F32)
             nc.gpsimd.memset(minus_half[:], -0.5)
-            n = 1
-            while n < HALF_E:
-                nc.vector.tensor_scalar(
-                    out=turns[:, n : 2 * n], in0=turns[:, 0:n], scalar1=FREQ_RATIO**n, scalar2=None,
-                    op0=ALU.mult,
-                )
-                n *= 2
-            low, high = slice(0, REDUCED), slice(REDUCED, HALF_E)
-            nc.vector.tensor_scalar(
-                out=whole, in0=turns[:, low], scalar1=ROUND, scalar2=ROUND, op0=ALU.add, op1=ALU.subtract
-            )
-            nc.vector.tensor_tensor(out=turns[:, low], in0=turns[:, low], in1=whole, op=ALU.subtract)
-            nc.vector.scalar_tensor_tensor(
-                out=abs_turns, in0=turns[:, low], scalar=-1.0, in1=turns[:, low], op0=ALU.mult, op1=ALU.max
-            )
-            for span, magnitudes in ((high, turns[:, high]), (low, abs_turns)):
-                nc.scalar.activation(
-                    out=cos_t[:, span], in_=turns[:, span], func=ACT.Sin, scale=2.0 * math.pi
-                )
-                nc.scalar.activation(
-                    out=cos_t[:, HALF_E + span.start : HALF_E + span.stop], in_=magnitudes, func=ACT.Sin,
-                    scale=-2.0 * math.pi, bias=math.pi / 2.0,
-                )
+            table_load = head.tile([P, 1], F32)
+            nc.scalar.activation(out=table_load[:], in_=pos[:], func=ACT.Sin, scale=1.0 / POSITIONS)
+            double_turns(1, 64)
 
-            transpose_slab(0)
-            nc.scalar.activation(out=sin_t[:, 0:HALF_E], in_=cos_t[:, 0:HALF_E], func=ACT.Sin, scale=-1.0)
-            nc.scalar.activation(out=sin_t[:, HALF_E:E], in_=cos_t[:, HALF_E:E], func=ACT.Sin)
-            transpose_slab(1)
-            nc.scalar.activation(out=cos_t[:], in_=cos_t[:], func=ACT.Sin, bias=math.pi / 2.0)
-            transpose_slab(2)
-            transpose_slab(3)
+            mean_var = head.tile([P, 2], F32)
+            stats = head.tile([P, D // 512, 6], F32)
+            for j in range(D // 512):
+                nc.vector.bn_stats(out=stats[:, j, :], in_=x_raw[0][:, j * 512 : (j + 1) * 512])
+            nc.vector.bn_aggr(out=mean_var[:], in_=stats[:].rearrange("p c s -> p (c s)"))
 
-            mean_var = head.tile([P, TOKEN_TILES, 2], F32)
-            for m in range(TOKEN_TILES):
-                stats = head.tile([P, D // 512, 6], F32, name="stats%d" % m)
-                for j in range(D // 512):
-                    nc.vector.bn_stats(out=stats[:, j, :], in_=x_raw[m][:, j * 512 : (j + 1) * 512])
-                nc.vector.bn_aggr(out=mean_var[:, m, :], in_=stats[:].rearrange("p c s -> p (c s)"))
-            rstd = []
-            for m in range(TOKEN_TILES):
-                rstd.append(head.tile([P, 1], F32, name="rstd%d" % m))
+            sums = head.tile([P, 1], F32)
+            minus_mean = head.tile([P, 1], F32)
+            square_sums = head.tile([P, 1], F32)
+            unused = head.tile([P, D], BF16)
+            nc.scalar.activation(out=unused[:], in_=x_raw[1][:], func=ACT.Copy, accum_out=sums[:])
+            nc.gpsimd.tensor_scalar(
+                out=minus_mean[:], in0=sums[:], scalar1=-1.0 / D, scalar2=0.0, op0=ALU.mult, op1=ALU.add
+            )
+            nc.scalar.activation(
+                out=unused[:], in_=x_raw[1][:], func=ACT.Square, bias=minus_mean[:], accum_out=square_sums[:]
+            )
+
+            def rstd_of(variance, factor, name):
+                rstd = head.tile([P, 1], F32, name=name)
                 nc.gpsimd.tensor_scalar(
-                    out=rstd[m][:], in0=mean_var[:, m, 1:2], scalar1=1.0, scalar2=EPS,
-                    op0=ALU.mult, op1=ALU.add,
+                    out=rstd[:], in0=variance, scalar1=factor, scalar2=EPS, op0=ALU.mult, op1=ALU.add
                 )
-                nc.gpsimd.tensor_tensor(out=rstd[m][:], in0=rstd[m][:], in1=minus_half[:], op=ALU.pow)
+                nc.gpsimd.tensor_tensor(out=rstd[:], in0=rstd[:], in1=minus_half[:], op=ALU.pow)
+                return rstd
+
+            rstds = [rstd_of(mean_var[:, 1:2], 1.0, "rstd0"), rstd_of(square_sums[:], 1.0 / D, "rstd1")]
             centred = []
-            xn = []
-            for m in range(TOKEN_TILES):
+            for m, (mean, op) in enumerate(((mean_var[:, 0:1], ALU.subtract), (minus_mean[:], ALU.add))):
                 centred.append(head.tile([P, D], F32, name="centred%d" % m))
                 nc.vector.scalar_tensor_tensor(
-                    out=centred[m][:], in0=x_raw[m][:], scalar=mean_var[:, m, 0:1], in1=gain_bc[:],
-                    op0=ALU.subtract, op1=ALU.mult,
+                    out=centred[m][:], in0=x_raw[m][:], scalar=mean, in1=gain_bc[:], op0=op, op1=ALU.mult
                 )
-                quantise_slab(m)
-            transpose_slab(4)
+            xn = []
             for m in range(TOKEN_TILES):
-                xn.append(head.tile([P, D], BF16, name="xn%d" % m))
-                nc.vector.scalar_tensor_tensor(
-                    out=xn[m][:], in0=centred[m][:], scalar=rstd[m][:], in1=shift_bc[:],
-                    op0=ALU.mult, op1=ALU.add,
-                )
-                quantise_slab(TOKEN_TILES + m)
-            transpose_slab(5)
+                xn.append(head.tile([P, PASSES, 2, WORDS_PER_PASS], BF16, name="xn%d" % m))
+                for u in range(2):
+                    by_word = "r (g p u e) -> r u g p e"
+                    nc.vector.scalar_tensor_tensor(
+                        out=xn[m][:, :, u, :].rearrange("r g (p e) -> r g p e", e=2),
+                        in0=centred[m][:].rearrange(by_word, g=PASSES, u=2, e=2)[:, u, :, :, :],
+                        scalar=rstds[m][:],
+                        in1=shift_bc[:].rearrange(by_word, g=PASSES, u=2, e=2)[:, u, :, :, :],
+                        op0=ALU.mult,
+                        op1=ALU.add,
+                    )
+
+            for slab in range(SLABS_BEFORE_X):
+                transpose_slab(slab)
+            quantise_slab(0)
+            double_turns(64, HALF_E)
+            reduce_turns()
 
             grouped_x = head.tile([P, PASSES * TOKENS * PACK], BF16, align_bytes=64)
-            grouped_x_words = grouped_x[:].bitcast(F32).rearrange("p (g r u) -> p g r u", g=PASSES, u=2)
+            dest_x = grouped_x[:].bitcast(F32).rearrange("p (g r u) -> p g r u", g=PASSES, u=2)
             for g in range(PASSES):
-                transpose_words(lambda m: xn[m][:], g * WORDS_PER_PASS, TOKENS, grouped_x_words[:, g, :, :])
-            quantise_slab(4)
+                transpose_words(lambda m, u: xn[m][:, g, u, :].bitcast(F32), TOKENS, dest_x[:, g, :, :])
             nc.vector.quantize_mx(out=x_codes[:].bitcast(FP8X4), scales=x_scales[:], in_=grouped_x[:])
-            quantise_slab(5)
 
-        for slab in range(6, SLABS_AHEAD):
-            transpose_slab(slab)
-            if slab > 6:
+            for slab in range(SLABS_BEFORE_X, SLABS_AHEAD):
                 quantise_slab(slab - 1)
+                transpose_slab(slab)
 
         rot = pools.enter_context(tc.tile_pool(name="rot", bufs=4))
 
@@ -246,13 +277,33 @@ def tile_rotaryembeddingtransformerlayer_pa_kernel(
             )
 
         def finish_v(c):
-            cc = c % CHUNKS_PER_OUTPUT
+            cc = c - FIRST_V
             for m in range(TOKEN_TILES):
                 v_rows = rot.tile([P, CHUNK], F32, name="v_rows")
                 add_bias(c, m, v_rows[:])
                 nc.sync.dma_start(
                     out=out_rows[2][m * P : (m + 1) * P, cc * CHUNK : (cc + 1) * CHUNK], in_=v_rows[:]
                 )
+
+        def multiply_by_sin(rows, rot_rows, j):
+            nc.vector.tensor_tensor(
+                out=rot_rows[:].rearrange("r (h j i) -> r h j i", h=2, j=2)[:, :, j, :],
+                in0=rows[:, j * HALF_E : (j + 1) * HALF_E].rearrange("r (i h) -> r h i", h=2),
+                in1=sin_t[:].rearrange("r (h j i) -> r h j i", h=2, j=2)[:, :, j, :],
+                op=ALU.mult,
+            )
+
+        def multiply_by_cos(rows, j):
+            span = slice(j * HALF_E, (j + 1) * HALF_E)
+            nc.vector.tensor_tensor(out=rows[:, span], in0=rows[:, span], in1=cos_t[:, span], op=ALU.mult)
+
+        def add_rotated(which, m, rows, rot_rows, span):
+            nc.vector.tensor_tensor(
+                out=rows[:, span], in0=rows[:, span], in1=rot_rows[:, span],
+                op=(ALU.add if which == 0 else ALU.subtract),
+            )
+            if span.stop == E:
+                nc.gpsimd.dma_start(out=out_rows[which][m * P : (m + 1) * P, :], in_=rows[:])
 
         def finish_q_or_k(c):
             which, cc = divmod(c, CHUNKS_PER_OUTPUT)
@@ -263,28 +314,22 @@ def tile_rotaryembeddingtransformerlayer_pa_kernel(
                 add_bias(c, m, q_rows[m][:, cc * CHUNK : (cc + 1) * CHUNK])
             if cc % 2 == 1:
                 j = cc // 2
-                span = slice(j * HALF_E, (j + 1) * HALF_E)
-                for m in range(TOKEN_TILES):
-                    nc.vector.tensor_tensor(
-                        out=mixed[m][:].rearrange("r (h j i) -> r h j i", h=2, j=2)[:, :, j, :],
-                        in0=q_rows[m][:, span].rearrange("r (i h) -> r h i", h=2),
-                        in1=sin_t[:].rearrange("r (h j i) -> r h j i", h=2, j=2)[:, :, j, :],
-                        op=ALU.mult,
-                    )
-                for m in range(TOKEN_TILES):
-                    nc.vector.tensor_tensor(
-                        out=q_rows[m][:, span], in0=q_rows[m][:, span], in1=cos_t[:, span], op=ALU.mult
-                    )
-            if cc == CHUNKS_PER_OUTPUT - 1:
-                for m in range(TOKEN_TILES):
-                    nc.vector.tensor_tensor(
-                        out=q_rows[m][:], in0=q_rows[m][:], in1=mixed[m][:],
-                        op=(ALU.add if which == 0 else ALU.subtract),
-                    )
-                    nc.gpsimd.dma_start(out=out_rows[which][m * P : (m + 1) * P, :], in_=q_rows[m][:])
+                ready = slice(0, CHUNK) if j == 0 else slice(CHUNK, E)
+                pairs = [(m, q_rows[m], mixed[m]) for m in range(TOKEN_TILES)]
+                for m, rows, rot_rows in pairs:
+                    mix_queue.append((multiply_by_sin, (rows, rot_rows, j)))
+                for m, rows, rot_rows in pairs:
+                    mix_queue.append((multiply_by_cos, (rows, j)))
+                for m, rows, rot_rows in pairs:
+                    mix_queue.append((add_rotated, (which, m, rows, rot_rows, ready)))
+
+        def mix(steps):
+            for step, args in mix_queue[:steps]:
+                step(*args)
+            mix_queue[:] = mix_queue[steps:]
 
         def multiply(slab):
-            c, part = divmod(slab, SLABS_PER_CHUNK)
+            part = slab % SLABS_PER_CHUNK
             for i in range(SLAB_PASSES):
                 g = part * SLAB_PASSES + i
                 for m in range(TOKEN_TILES):
@@ -301,15 +346,19 @@ def tile_rotaryembeddingtransformerlayer_pa_kernel(
                         stop=(g == PASSES - 1),
                     )
 
+        tables = [fill_emb, fill_sin, fill_cos]
         for slab in range(SLABS_AHEAD, SLABS + SLABS_AHEAD):
             multiply(slab - SLABS_AHEAD)
             if slab < SLABS:
                 transpose_slab(slab)
+            if slab - SLABS_AHEAD < len(tables):
+                tables[slab - SLABS_AHEAD]()
             if slab <= SLABS:
                 quantise_slab(slab - 1)
-            c, part = divmod(slab - SLABS_AHEAD, SLABS_PER_CHUNK)
+            i, part = divmod(slab - SLABS_AHEAD, SLABS_PER_CHUNK)
             if part == SLABS_PER_CHUNK - 1:
-                if c < 2 * CHUNKS_PER_OUTPUT:
-                    finish_q_or_k(c)
+                if ORDER[i] < FIRST_V:
+                    finish_q_or_k(ORDER[i])
                 else:
-                    finish_v(c)
+                    finish_v(ORDER[i])
+            mix(MIX_STEPS)

@@ -46,6 +46,7 @@ SLABS = CHUNKS * SLABS_PER_CHUNK
 SLABS_AHEAD = 3
 SLABS_BEFORE_X = 2
 W_BUFS = 5
+SORTED_TILES = 1
 MIX_STEPS = 2
 GROUPED_BUFS = 4
 CODE_BUFS = SLABS_AHEAD + 2
@@ -69,6 +70,7 @@ def tile_rotaryembeddingtransformerlayer_pa_kernel(
         const = pools.enter_context(tc.tile_pool(name="const", bufs=1))
         w_pool = pools.enter_context(tc.tile_pool(name="w_raw", bufs=W_BUFS))
         grouped_pool = pools.enter_context(tc.tile_pool(name="grouped", bufs=GROUPED_BUFS))
+        sorted_pool = pools.enter_context(tc.tile_pool(name="sorted", bufs=2))
         code_pool = pools.enter_context(tc.tile_pool(name="codes", bufs=CODE_BUFS))
         psum_tr = pools.enter_context(tc.psum_pool(name="psum_tr", bufs=4))
         psum_acc = pools.enter_context(tc.psum_pool(name="psum_acc", bufs=4))
@@ -81,6 +83,7 @@ def tile_rotaryembeddingtransformerlayer_pa_kernel(
         sin_t = const.tile([P, E], F32)
 
         w_raw = {}
+        w_sorted = {}
         grouped = {}
         w_codes = {}
         w_scales = {}
@@ -111,17 +114,35 @@ def tile_rotaryembeddingtransformerlayer_pa_kernel(
                     nc.tensor.transpose(w_t[:, u, j * P : (j + 1) * P], words_of(j, u), ident[:])
             nc.scalar.copy(out=dest_words, in_=w_t[:].rearrange("p u n -> p n u"))
 
+        def sort_slab(slab):
+            i, part = divmod(slab, SLABS_PER_CHUNK)
+            words = slice(part * SLAB_WORDS, (part + 1) * SLAB_WORDS)
+            w_sorted[slab] = sorted_pool.tile([P, SORTED_TILES, SLAB_PASSES, 2, P], F32, name="w_sorted")
+            for t in range(SORTED_TILES):
+                nc.scalar.copy(
+                    out=w_sorted[slab][:, t, :, :, :],
+                    in_=w_raw[i][:, t, :].bitcast(F32)[:, words].rearrange("r (g p u) -> r g u p", p=P, u=2),
+                )
+
         def transpose_slab(slab):
             i, part = divmod(slab, SLABS_PER_CHUNK)
             grouped[slab] = grouped_pool.tile(
                 [P, SLAB_PASSES * CHUNK * PACK], BF16, name="grouped", align_bytes=64
             )
             dest = grouped[slab][:].bitcast(F32).rearrange("p (g n u) -> p g n u", g=SLAB_PASSES, u=2)
-            for g in range(SLAB_PASSES):
+
+            def words_of(g, t, u):
+                if t < SORTED_TILES:
+                    return w_sorted[slab][:, t, g, u, :]
                 w0 = part * SLAB_WORDS + g * WORDS_PER_PASS
+                return w_raw[i][:, t, :].bitcast(F32)[:, w0 + u : w0 + WORDS_PER_PASS : 2]
+
+            if slab + 1 < SLABS:
+                sort_slab(slab + 1)
+            for g in range(SLAB_PASSES):
                 for h in range(2):
                     transpose_words(
-                        lambda j, u: w_raw[i][:, 2 * h + j, :].bitcast(F32)[:, w0 + u : w0 + WORDS_PER_PASS : 2],
+                        lambda j, u: words_of(g, 2 * h + j, u),
                         2 * P,
                         dest[:, g, h * 2 * P : (h + 1) * 2 * P, :],
                     )
@@ -155,21 +176,32 @@ def tile_rotaryembeddingtransformerlayer_pa_kernel(
             )
             nc.vector.tensor_tensor(out=low, in0=low, in1=whole, op=ALU.subtract)
 
-        def fill_emb():
+        def fill_emb_sin():
             nc.scalar.activation(out=cos_t[:, 0:HALF_E], in_=turns, func=ACT.Sin, scale=2.0 * math.pi)
+
+        def fill_emb_cos():
             nc.scalar.activation(out=abs_turns, in_=turns[:, 0:REDUCED], func=ACT.Abs)
-            for first, magnitudes in ((0, abs_turns), (REDUCED, turns[:, REDUCED:HALF_E])):
+            for first, magnitudes in ((REDUCED, turns[:, REDUCED:HALF_E]), (0, abs_turns)):
                 nc.scalar.activation(
                     out=cos_t[:, HALF_E + first : HALF_E + first + REDUCED], in_=magnitudes, func=ACT.Sin,
                     scale=-2.0 * math.pi, bias=math.pi / 2.0,
                 )
 
-        def fill_sin():
-            nc.scalar.activation(out=sin_t[:, 0:HALF_E], in_=cos_t[:, 0:HALF_E], func=ACT.Sin, scale=-1.0)
-            nc.scalar.activation(out=sin_t[:, HALF_E:E], in_=cos_t[:, HALF_E:E], func=ACT.Sin)
+        def fill_sin(half, sign):
+            nc.scalar.activation(out=sin_t[:, half], in_=cos_t[:, half], func=ACT.Sin, scale=sign)
 
-        def fill_cos():
-            nc.scalar.activation(out=cos_t[:], in_=cos_t[:], func=ACT.Sin, bias=math.pi / 2.0)
+        def fill_cos(half):
+            nc.scalar.activation(out=cos_t[:, half], in_=cos_t[:, half], func=ACT.Sin, bias=math.pi / 2.0)
+
+        first_half, second_half = slice(0, HALF_E), slice(HALF_E, E)
+        table_steps = [
+            (fill_emb_sin, ()),
+            (fill_emb_cos, ()),
+            (fill_sin, (first_half, -1.0)),
+            (fill_sin, (second_half, 1.0)),
+            (fill_cos, (first_half,)),
+            (fill_cos, (second_half,)),
+        ]
 
         with tc.tile_pool(name="head", bufs=1) as head:
             x_raw = []
@@ -250,6 +282,7 @@ def tile_rotaryembeddingtransformerlayer_pa_kernel(
                         op1=ALU.add,
                     )
 
+            sort_slab(0)
             for slab in range(SLABS_BEFORE_X):
                 transpose_slab(slab)
             quantise_slab(0)
@@ -303,7 +336,7 @@ def tile_rotaryembeddingtransformerlayer_pa_kernel(
                 op=(ALU.add if which == 0 else ALU.subtract),
             )
             if span.stop == E:
-                nc.gpsimd.dma_start(out=out_rows[which][m * P : (m + 1) * P, :], in_=rows[:])
+                nc.sync.dma_start(out=out_rows[which][m * P : (m + 1) * P, :], in_=rows[:])
 
         def finish_q_or_k(c):
             which, cc = divmod(c, CHUNKS_PER_OUTPUT)
@@ -346,13 +379,13 @@ def tile_rotaryembeddingtransformerlayer_pa_kernel(
                         stop=(g == PASSES - 1),
                     )
 
-        tables = [fill_emb, fill_sin, fill_cos]
         for slab in range(SLABS_AHEAD, SLABS + SLABS_AHEAD):
             multiply(slab - SLABS_AHEAD)
             if slab < SLABS:
                 transpose_slab(slab)
-            if slab - SLABS_AHEAD < len(tables):
-                tables[slab - SLABS_AHEAD]()
+            if slab - SLABS_AHEAD < len(table_steps):
+                step, args = table_steps[slab - SLABS_AHEAD]
+                step(*args)
             if slab <= SLABS:
                 quantise_slab(slab - 1)
             i, part = divmod(slab - SLABS_AHEAD, SLABS_PER_CHUNK)

@@ -46,10 +46,12 @@ SLABS = CHUNKS * SLABS_PER_CHUNK
 SLABS_AHEAD = 3
 SLABS_BEFORE_X = 2
 W_BUFS = 5
-SORTED_TILES = 1
 MIX_STEPS = 2
 GROUPED_BUFS = 4
 CODE_BUFS = SLABS_AHEAD + 2
+
+GAIN_PIECE, SHIFT_PIECE, BIAS_PIECE = 0, D // CHUNK, 2 * D // CHUNK
+PIECES = BIAS_PIECE + CHUNKS
 
 ROUND = 1.5 * 2.0**23
 FREQ_RATIO = 10000.0 ** (-1.0 / HALF_E)
@@ -70,20 +72,21 @@ def tile_rotaryembeddingtransformerlayer_pa_kernel(
         const = pools.enter_context(tc.tile_pool(name="const", bufs=1))
         w_pool = pools.enter_context(tc.tile_pool(name="w_raw", bufs=W_BUFS))
         grouped_pool = pools.enter_context(tc.tile_pool(name="grouped", bufs=GROUPED_BUFS))
-        sorted_pool = pools.enter_context(tc.tile_pool(name="sorted", bufs=2))
         code_pool = pools.enter_context(tc.tile_pool(name="codes", bufs=CODE_BUFS))
+        bias_pool = pools.enter_context(tc.tile_pool(name="bias", bufs=3))
         psum_tr = pools.enter_context(tc.psum_pool(name="psum_tr", bufs=4))
         psum_acc = pools.enter_context(tc.psum_pool(name="psum_acc", bufs=4))
 
         ident = const.tile([P, P], F32)
-        bias_bc = const.tile([P, 3 * E], BF16)
+        vectors = const.tile([P, CHUNK], BF16)
+        select = const.tile([P, PIECES], BF16)
         x_codes = const.tile([P, PASSES * TOKENS], U32, align_bytes=64)
         x_scales = const.tile([P, PASSES * TOKENS], U8, align_bytes=64)
         cos_t = const.tile([P, E], F32)
         sin_t = const.tile([P, E], F32)
 
+        bias_bc = {}
         w_raw = {}
-        w_sorted = {}
         grouped = {}
         w_codes = {}
         w_scales = {}
@@ -99,30 +102,30 @@ def tile_rotaryembeddingtransformerlayer_pa_kernel(
                 k = slice(part * (D // parts), (part + 1) * (D // parts))
                 nc.sync.dma_start(
                     out=w_raw[i][:, :, k],
-                    in_=Wqkv[c * CHUNK : (c + 1) * CHUNK, k].rearrange("(p t) k -> p t k", t=ROW_TILES),
+                    in_=Wqkv[c * CHUNK : (c + 1) * CHUNK, k].rearrange("(t p) k -> p t k", t=ROW_TILES),
                 )
-                if i == 0 and part == 0:
-                    nc.sync.dma_start(out=shift_bc[:], in_=be1.partition_broadcast(P))
-            if c in (FIRST_Q, FIRST_K, FIRST_V):
-                span = slice(c * CHUNK, c * CHUNK + E)
-                nc.sync.dma_start(out=bias_bc[:, span], in_=bqkv[span].partition_broadcast(P))
 
-        def transpose_words(words_of, width, dest_words):
+        def spread(piece, dest):
+            nc.tensor.matmul(
+                dest, lhsT=select[:, piece : piece + 1].to_broadcast([P, P]), rhs=vectors[:],
+                start=True, stop=True,
+            )
+
+        def spread_bias(i):
+            c = ORDER[i]
+            bias_bc[c] = bias_pool.tile([P, CHUNK], BF16, name="bias_bc")
+            spread_out = psum_tr.tile([P, CHUNK], F32, name="spread_out", tag="tr")
+            spread(BIAS_PIECE + c, spread_out[:])
+            nc.scalar.copy(out=bias_bc[c][:], in_=spread_out[:])
+
+        def transpose_words(rows_of, w0, width, dest_words):
             w_t = psum_tr.tile([P, 2, width], F32, name="w_t", tag="tr")
             for j in range(width // P):
+                words = rows_of(j).bitcast(F32)
                 for u in range(2):
-                    nc.tensor.transpose(w_t[:, u, j * P : (j + 1) * P], words_of(j, u), ident[:])
+                    pair = slice(w0 + u, w0 + WORDS_PER_PASS, 2)
+                    nc.tensor.transpose(w_t[:, u, j * P : (j + 1) * P], words[:, pair], ident[:])
             nc.scalar.copy(out=dest_words, in_=w_t[:].rearrange("p u n -> p n u"))
-
-        def sort_slab(slab):
-            i, part = divmod(slab, SLABS_PER_CHUNK)
-            words = slice(part * SLAB_WORDS, (part + 1) * SLAB_WORDS)
-            w_sorted[slab] = sorted_pool.tile([P, SORTED_TILES, SLAB_PASSES, 2, P], F32, name="w_sorted")
-            for t in range(SORTED_TILES):
-                nc.scalar.copy(
-                    out=w_sorted[slab][:, t, :, :, :],
-                    in_=w_raw[i][:, t, :].bitcast(F32)[:, words].rearrange("r (g p u) -> r g u p", p=P, u=2),
-                )
 
         def transpose_slab(slab):
             i, part = divmod(slab, SLABS_PER_CHUNK)
@@ -130,19 +133,11 @@ def tile_rotaryembeddingtransformerlayer_pa_kernel(
                 [P, SLAB_PASSES * CHUNK * PACK], BF16, name="grouped", align_bytes=64
             )
             dest = grouped[slab][:].bitcast(F32).rearrange("p (g n u) -> p g n u", g=SLAB_PASSES, u=2)
-
-            def words_of(g, t, u):
-                if t < SORTED_TILES:
-                    return w_sorted[slab][:, t, g, u, :]
-                w0 = part * SLAB_WORDS + g * WORDS_PER_PASS
-                return w_raw[i][:, t, :].bitcast(F32)[:, w0 + u : w0 + WORDS_PER_PASS : 2]
-
-            if slab + 1 < SLABS:
-                sort_slab(slab + 1)
             for g in range(SLAB_PASSES):
                 for h in range(2):
                     transpose_words(
-                        lambda j, u: words_of(g, 2 * h + j, u),
+                        lambda j: w_raw[i][:, 2 * h + j, :],
+                        part * SLAB_WORDS + g * WORDS_PER_PASS,
                         2 * P,
                         dest[:, g, h * 2 * P : (h + 1) * 2 * P, :],
                     )
@@ -204,13 +199,16 @@ def tile_rotaryembeddingtransformerlayer_pa_kernel(
         ]
 
         with tc.tile_pool(name="head", bufs=1) as head:
+            nc.vector.memset(vectors[:], 0.0)
+            for piece, vector in ((GAIN_PIECE, g1), (SHIFT_PIECE, be1), (BIAS_PIECE, bqkv)):
+                nc.scalar.dma_start(
+                    out=vectors[piece : piece + vector.shape[0] // CHUNK, :],
+                    in_=vector.rearrange("(r n) -> r n", n=CHUNK),
+                )
             x_raw = []
             for m in range(TOKEN_TILES):
                 x_raw.append(head.tile([P, D], BF16, name="x_raw%d" % m))
                 nc.sync.dma_start(out=x_raw[m][:], in_=x_rows[m * P : (m + 1) * P, :])
-            gain_bc = head.tile([P, D], BF16)
-            nc.sync.dma_start(out=gain_bc[:], in_=g1.partition_broadcast(P))
-            shift_bc = head.tile([P, D], BF16)
             load_chunk(0, SLABS_PER_CHUNK)
             for i in range(1, W_BUFS):
                 load_chunk(i, 1)
@@ -229,6 +227,7 @@ def tile_rotaryembeddingtransformerlayer_pa_kernel(
                 op0=ALU.mult, op1=ALU.add,
             )
             make_identity(nc, ident[:])
+            nc.vector.tensor_copy(out=select[:], in_=ident[:, 0:PIECES])
             minus_half = head.tile([P, 1], F32)
             nc.gpsimd.memset(minus_half[:], -0.5)
             table_load = head.tile([P, 1], F32)
@@ -262,29 +261,37 @@ def tile_rotaryembeddingtransformerlayer_pa_kernel(
                 return rstd
 
             rstds = [rstd_of(mean_var[:, 1:2], 1.0, "rstd0"), rstd_of(square_sums[:], 1.0 / D, "rstd1")]
+            def spread_to_banks(first_piece):
+                banks = []
+                for j in range(D // CHUNK):
+                    bank = psum_acc.tile([P, CHUNK], F32, name="bank", tag="acc")
+                    spread(first_piece + j, bank[:])
+                    banks.append(bank)
+                return banks
+
+            gain_banks = spread_to_banks(GAIN_PIECE)
+            transpose_slab(0)
+            pieces = [slice(j * CHUNK, (j + 1) * CHUNK) for j in range(D // CHUNK)]
             centred = []
             for m, (mean, op) in enumerate(((mean_var[:, 0:1], ALU.subtract), (minus_mean[:], ALU.add))):
                 centred.append(head.tile([P, D], F32, name="centred%d" % m))
-                nc.vector.scalar_tensor_tensor(
-                    out=centred[m][:], in0=x_raw[m][:], scalar=mean, in1=gain_bc[:], op0=op, op1=ALU.mult
-                )
+                for j, piece in enumerate(pieces):
+                    nc.vector.scalar_tensor_tensor(
+                        out=centred[m][:, piece], in0=x_raw[m][:, piece], scalar=mean, in1=gain_banks[j][:],
+                        op0=op, op1=ALU.mult,
+                    )
+            shift_banks = spread_to_banks(SHIFT_PIECE)
             xn = []
             for m in range(TOKEN_TILES):
-                xn.append(head.tile([P, PASSES, 2, WORDS_PER_PASS], BF16, name="xn%d" % m))
-                for u in range(2):
-                    by_word = "r (g p u e) -> r u g p e"
+                xn.append(head.tile([P, D], BF16, name="xn%d" % m))
+                for j, piece in enumerate(pieces):
                     nc.vector.scalar_tensor_tensor(
-                        out=xn[m][:, :, u, :].rearrange("r g (p e) -> r g p e", e=2),
-                        in0=centred[m][:].rearrange(by_word, g=PASSES, u=2, e=2)[:, u, :, :, :],
-                        scalar=rstds[m][:],
-                        in1=shift_bc[:].rearrange(by_word, g=PASSES, u=2, e=2)[:, u, :, :, :],
-                        op0=ALU.mult,
-                        op1=ALU.add,
+                        out=xn[m][:, piece], in0=centred[m][:, piece], scalar=rstds[m][:],
+                        in1=shift_banks[j][:], op0=ALU.mult, op1=ALU.add,
                     )
-
-            sort_slab(0)
-            for slab in range(SLABS_BEFORE_X):
+            for slab in range(1, SLABS_BEFORE_X):
                 transpose_slab(slab)
+            spread_bias(0)
             quantise_slab(0)
             double_turns(64, HALF_E)
             reduce_turns()
@@ -292,7 +299,7 @@ def tile_rotaryembeddingtransformerlayer_pa_kernel(
             grouped_x = head.tile([P, PASSES * TOKENS * PACK], BF16, align_bytes=64)
             dest_x = grouped_x[:].bitcast(F32).rearrange("p (g r u) -> p g r u", g=PASSES, u=2)
             for g in range(PASSES):
-                transpose_words(lambda m, u: xn[m][:, g, u, :].bitcast(F32), TOKENS, dest_x[:, g, :, :])
+                transpose_words(lambda m: xn[m][:], g * WORDS_PER_PASS, TOKENS, dest_x[:, g, :, :])
             nc.vector.quantize_mx(out=x_codes[:].bitcast(FP8X4), scales=x_scales[:], in_=grouped_x[:])
 
             for slab in range(SLABS_BEFORE_X, SLABS_AHEAD):
@@ -302,12 +309,7 @@ def tile_rotaryembeddingtransformerlayer_pa_kernel(
         rot = pools.enter_context(tc.tile_pool(name="rot", bufs=4))
 
         def add_bias(c, m, dest):
-            nc.vector.tensor_tensor(
-                out=dest.rearrange("r (p t) -> r p t", t=ROW_TILES),
-                in0=acc[m][:].rearrange("r (t p) -> r p t", t=ROW_TILES),
-                in1=bias_bc[:, c * CHUNK : (c + 1) * CHUNK].rearrange("r (p t) -> r p t", t=ROW_TILES),
-                op=ALU.add,
-            )
+            nc.vector.tensor_tensor(out=dest, in0=acc[m][:], in1=bias_bc[c][:], op=ALU.add)
 
         def finish_v(c):
             cc = c - FIRST_V
@@ -381,6 +383,8 @@ def tile_rotaryembeddingtransformerlayer_pa_kernel(
 
         for slab in range(SLABS_AHEAD, SLABS + SLABS_AHEAD):
             multiply(slab - SLABS_AHEAD)
+            if slab % SLABS_PER_CHUNK == 0 and slab <= SLABS:
+                spread_bias(slab // SLABS_PER_CHUNK - 1)
             if slab < SLABS:
                 transpose_slab(slab)
             if slab - SLABS_AHEAD < len(table_steps):

@@ -30,28 +30,28 @@ CHUNK = 512
 ROW_TILES = CHUNK // P
 CHUNKS = 3 * E // CHUNK
 CHUNKS_PER_OUTPUT = E // CHUNK
-FIRST_Q, FIRST_K, FIRST_V = 0, CHUNKS_PER_OUTPUT, 2 * CHUNKS_PER_OUTPUT
-ORDER = (
-    [FIRST_V]
-    + list(range(FIRST_Q, FIRST_K))
-    + [FIRST_V + 1]
-    + list(range(FIRST_K, FIRST_V))
-    + [FIRST_V + 2, FIRST_V + 3]
-)
+FIRST_V = 2 * CHUNKS_PER_OUTPUT
 SLAB_PASSES = 2
 SLAB_K = SLAB_PASSES * K_PASS
-SLAB_WORDS = SLAB_K // 2
 SLABS_PER_CHUNK = PASSES // SLAB_PASSES
 SLABS = CHUNKS * SLABS_PER_CHUNK
-SLABS_AHEAD = 3
-SLABS_BEFORE_X = 2
-W_BUFS = 5
+SLABS_AHEAD = 6
+AHEAD = 3
+SLABS_BEFORE_SHIFT = 2
+SLABS_BEFORE_X = 4
+W_BUFS = 8
+SORTED = (1, 1)
+SORT_FROM = 6
+EARLY_TABLE_STEPS = 2
 MIX_STEPS = 2
-GROUPED_BUFS = 4
-CODE_BUFS = SLABS_AHEAD + 2
+GROUPED_BUFS = 6
+QUANTISE_AHEAD = 2
+CODE_BUFS = QUANTISE_AHEAD + 2
+QUANTISED_BEFORE_X = 2
 
-GAIN_PIECE, SHIFT_PIECE, BIAS_PIECE = 0, D // CHUNK, 2 * D // CHUNK
-PIECES = BIAS_PIECE + CHUNKS
+PIECE = 256
+GAIN_PIECE, SHIFT_PIECE = 0, D // PIECE
+PIECES = 2 * D // PIECE
 
 ROUND = 1.5 * 2.0**23
 FREQ_RATIO = 10000.0 ** (-1.0 / HALF_E)
@@ -72,21 +72,22 @@ def tile_rotaryembeddingtransformerlayer_pa_kernel(
         const = pools.enter_context(tc.tile_pool(name="const", bufs=1))
         w_pool = pools.enter_context(tc.tile_pool(name="w_raw", bufs=W_BUFS))
         grouped_pool = pools.enter_context(tc.tile_pool(name="grouped", bufs=GROUPED_BUFS))
+        sorted_pool = pools.enter_context(tc.tile_pool(name="sorted", bufs=2))
         code_pool = pools.enter_context(tc.tile_pool(name="codes", bufs=CODE_BUFS))
-        bias_pool = pools.enter_context(tc.tile_pool(name="bias", bufs=3))
         psum_tr = pools.enter_context(tc.psum_pool(name="psum_tr", bufs=4))
         psum_acc = pools.enter_context(tc.psum_pool(name="psum_acc", bufs=4))
 
         ident = const.tile([P, P], F32)
-        vectors = const.tile([P, CHUNK], BF16)
+        vectors = const.tile([P, PIECE], BF16)
+        bias_bc = const.tile([P, 3 * E], BF16)
         select = const.tile([P, PIECES], BF16)
         x_codes = const.tile([P, PASSES * TOKENS], U32, align_bytes=64)
         x_scales = const.tile([P, PASSES * TOKENS], U8, align_bytes=64)
         cos_t = const.tile([P, E], F32)
         sin_t = const.tile([P, E], F32)
 
-        bias_bc = {}
         w_raw = {}
+        w_sorted = {}
         grouped = {}
         w_codes = {}
         w_scales = {}
@@ -95,15 +96,21 @@ def tile_rotaryembeddingtransformerlayer_pa_kernel(
         mixed = {}
         mix_queue = []
 
-        def load_chunk(i, parts):
-            c = ORDER[i]
-            w_raw[i] = w_pool.tile([P, ROW_TILES, D], BF16, name="w_raw")
-            for part in range(parts):
-                k = slice(part * (D // parts), (part + 1) * (D // parts))
+        def load_slab(slab, parts):
+            c, part = divmod(slab, SLABS_PER_CHUNK)
+            w_raw[slab] = w_pool.tile([P, ROW_TILES, SLAB_K], BF16, name="w_raw")
+            n = ROW_TILES // parts
+            for h in range(parts):
                 nc.sync.dma_start(
-                    out=w_raw[i][:, :, k],
-                    in_=Wqkv[c * CHUNK : (c + 1) * CHUNK, k].rearrange("(t p) k -> p t k", t=ROW_TILES),
+                    out=w_raw[slab][:, h * n : (h + 1) * n, :],
+                    in_=Wqkv[
+                        c * CHUNK + h * n * P : c * CHUNK + (h + 1) * n * P, part * SLAB_K : (part + 1) * SLAB_K
+                    ].rearrange("(t p) k -> p t k", t=n),
                 )
+
+        def load_bias(c):
+            span = slice(c * CHUNK, (c + 1) * CHUNK)
+            nc.sync.dma_start(out=bias_bc[:, span], in_=bqkv[span].partition_broadcast(P))
 
         def spread(piece, dest):
             nc.tensor.matmul(
@@ -111,38 +118,52 @@ def tile_rotaryembeddingtransformerlayer_pa_kernel(
                 start=True, stop=True,
             )
 
-        def spread_bias(i):
-            c = ORDER[i]
-            bias_bc[c] = bias_pool.tile([P, CHUNK], BF16, name="bias_bc")
-            spread_out = psum_tr.tile([P, CHUNK], F32, name="spread_out", tag="tr")
-            spread(BIAS_PIECE + c, spread_out[:])
-            nc.scalar.copy(out=bias_bc[c][:], in_=spread_out[:])
+        def every_second_word(row, w0, u):
+            return row.bitcast(F32)[:, w0 + u : w0 + WORDS_PER_PASS : 2]
 
-        def transpose_words(rows_of, w0, width, dest_words):
+        def transpose_words(words_of, width, dest_words):
             w_t = psum_tr.tile([P, 2, width], F32, name="w_t", tag="tr")
             for j in range(width // P):
-                words = rows_of(j).bitcast(F32)
                 for u in range(2):
-                    pair = slice(w0 + u, w0 + WORDS_PER_PASS, 2)
-                    nc.tensor.transpose(w_t[:, u, j * P : (j + 1) * P], words[:, pair], ident[:])
+                    nc.tensor.transpose(w_t[:, u, j * P : (j + 1) * P], words_of(j, u), ident[:])
             nc.scalar.copy(out=dest_words, in_=w_t[:].rearrange("p u n -> p n u"))
 
+        def sort_slab(slab):
+            for g, tiles in enumerate(SORTED):
+                if tiles:
+                    w0 = g * WORDS_PER_PASS
+                    w_sorted[slab, g] = sorted_pool.tile([P, tiles, 2, P], F32, name="w_sorted%d" % g)
+                    nc.scalar.copy(
+                        out=w_sorted[slab, g][:],
+                        in_=w_raw[slab][:, 0:tiles, 2 * w0 : 2 * (w0 + WORDS_PER_PASS)].bitcast(F32).rearrange(
+                            "r t (p u) -> r t u p", u=2
+                        ),
+                    )
+
         def transpose_slab(slab):
-            i, part = divmod(slab, SLABS_PER_CHUNK)
             grouped[slab] = grouped_pool.tile(
                 [P, SLAB_PASSES * CHUNK * PACK], BF16, name="grouped", align_bytes=64
             )
             dest = grouped[slab][:].bitcast(F32).rearrange("p (g n u) -> p g n u", g=SLAB_PASSES, u=2)
+
+            def words_of(g, t, u):
+                if (slab, g) in w_sorted and t < SORTED[g]:
+                    return w_sorted[slab, g][:, t, u, :]
+                return every_second_word(w_raw[slab][:, t, :], g * WORDS_PER_PASS, u)
+
+            if SORT_FROM <= slab + 1 < SLABS:
+                sort_slab(slab + 1)
             for g in range(SLAB_PASSES):
                 for h in range(2):
                     transpose_words(
-                        lambda j: w_raw[i][:, 2 * h + j, :],
-                        part * SLAB_WORDS + g * WORDS_PER_PASS,
+                        lambda j, u: words_of(g, 2 * h + j, u),
                         2 * P,
                         dest[:, g, h * 2 * P : (h + 1) * 2 * P, :],
                     )
-            if part == SLABS_PER_CHUNK - 1 and i + W_BUFS < CHUNKS:
-                load_chunk(i + W_BUFS, 1)
+            if slab + W_BUFS < SLABS:
+                load_slab(slab + W_BUFS, 1)
+            if slab % SLABS_PER_CHUNK == 0:
+                load_bias(slab // SLABS_PER_CHUNK)
 
         def quantise_slab(slab):
             w_codes[slab] = code_pool.tile([P, SLAB_PASSES * CHUNK], U32, name="w_codes", align_bytes=64)
@@ -199,19 +220,21 @@ def tile_rotaryembeddingtransformerlayer_pa_kernel(
         ]
 
         with tc.tile_pool(name="head", bufs=1) as head:
-            nc.vector.memset(vectors[:], 0.0)
-            for piece, vector in ((GAIN_PIECE, g1), (SHIFT_PIECE, be1), (BIAS_PIECE, bqkv)):
-                nc.scalar.dma_start(
-                    out=vectors[piece : piece + vector.shape[0] // CHUNK, :],
-                    in_=vector.rearrange("(r n) -> r n", n=CHUNK),
-                )
+            nc.vector.memset(vectors[:].bitcast(F32), 0.0)
             x_raw = []
             for m in range(TOKEN_TILES):
                 x_raw.append(head.tile([P, D], BF16, name="x_raw%d" % m))
+            def load_x(m):
                 nc.sync.dma_start(out=x_raw[m][:], in_=x_rows[m * P : (m + 1) * P, :])
-            load_chunk(0, SLABS_PER_CHUNK)
-            for i in range(1, W_BUFS):
-                load_chunk(i, 1)
+            load_x(0)
+            for piece, vector in ((GAIN_PIECE, g1), (SHIFT_PIECE, be1)):
+                nc.sync.dma_start(
+                    out=vectors[piece : piece + D // PIECE, :], in_=vector.rearrange("(r n) -> r n", n=PIECE)
+                )
+            load_x(1)
+            load_slab(0, 2)
+            for slab in range(1, W_BUFS):
+                load_slab(slab, 1)
 
             pos = head.tile([P, 1], F32)
             for first in range(0, P, POSITIONS):
@@ -227,89 +250,84 @@ def tile_rotaryembeddingtransformerlayer_pa_kernel(
                 op0=ALU.mult, op1=ALU.add,
             )
             make_identity(nc, ident[:])
-            nc.vector.tensor_copy(out=select[:], in_=ident[:, 0:PIECES])
             minus_half = head.tile([P, 1], F32)
             nc.gpsimd.memset(minus_half[:], -0.5)
             table_load = head.tile([P, 1], F32)
             nc.scalar.activation(out=table_load[:], in_=pos[:], func=ACT.Sin, scale=1.0 / POSITIONS)
-            double_turns(1, 64)
+            double_turns(1, HALF_E)
+            reduce_turns()
+            nc.vector.tensor_copy(out=select[:], in_=ident[:, 0:PIECES])
+            for step, args in table_steps[:EARLY_TABLE_STEPS]:
+                step(*args)
 
-            mean_var = head.tile([P, 2], F32)
-            stats = head.tile([P, D // 512, 6], F32)
-            for j in range(D // 512):
-                nc.vector.bn_stats(out=stats[:, j, :], in_=x_raw[0][:, j * 512 : (j + 1) * 512])
-            nc.vector.bn_aggr(out=mean_var[:], in_=stats[:].rearrange("p c s -> p (c s)"))
+            mean = []
+            rstd = []
 
-            sums = head.tile([P, 1], F32)
-            minus_mean = head.tile([P, 1], F32)
-            square_sums = head.tile([P, 1], F32)
-            unused = head.tile([P, D], BF16)
-            nc.scalar.activation(out=unused[:], in_=x_raw[1][:], func=ACT.Copy, accum_out=sums[:])
-            nc.gpsimd.tensor_scalar(
-                out=minus_mean[:], in0=sums[:], scalar1=-1.0 / D, scalar2=0.0, op0=ALU.mult, op1=ALU.add
-            )
-            nc.scalar.activation(
-                out=unused[:], in_=x_raw[1][:], func=ACT.Square, bias=minus_mean[:], accum_out=square_sums[:]
-            )
-
-            def rstd_of(variance, factor, name):
-                rstd = head.tile([P, 1], F32, name=name)
+            def take_rstd(m, variance):
+                rstd.append(head.tile([P, 1], F32, name="rstd%d" % m))
                 nc.gpsimd.tensor_scalar(
-                    out=rstd[:], in0=variance, scalar1=factor, scalar2=EPS, op0=ALU.mult, op1=ALU.add
+                    out=rstd[m][:], in0=variance, scalar1=1.0, scalar2=EPS, op0=ALU.mult, op1=ALU.add
                 )
-                nc.gpsimd.tensor_tensor(out=rstd[:], in0=rstd[:], in1=minus_half[:], op=ALU.pow)
-                return rstd
+                nc.gpsimd.tensor_tensor(out=rstd[m][:], in0=rstd[m][:], in1=minus_half[:], op=ALU.pow)
 
-            rstds = [rstd_of(mean_var[:, 1:2], 1.0, "rstd0"), rstd_of(square_sums[:], 1.0 / D, "rstd1")]
+            def take_stats(m):
+                stats = head.tile([P, D // 512, 6], F32, name="stats%d" % m)
+                mean_var = head.tile([P, 2], F32, name="mean_var%d" % m)
+                for j in range(D // 512):
+                    nc.vector.bn_stats(out=stats[:, j, :], in_=x_raw[m][:, j * 512 : (j + 1) * 512])
+                nc.vector.bn_aggr(out=mean_var[:], in_=stats[:].rearrange("p c s -> p (c s)"))
+                mean.append(mean_var[:, 0:1])
+                take_rstd(m, mean_var[:, 1:2])
+
             def spread_to_banks(first_piece):
                 banks = []
                 for j in range(D // CHUNK):
                     bank = psum_acc.tile([P, CHUNK], F32, name="bank", tag="acc")
-                    spread(first_piece + j, bank[:])
+                    for h in range(CHUNK // PIECE):
+                        spread(first_piece + j * (CHUNK // PIECE) + h, bank[:, h * PIECE : (h + 1) * PIECE])
                     banks.append(bank)
                 return banks
 
+            for m in range(TOKEN_TILES):
+                take_stats(m)
             gain_banks = spread_to_banks(GAIN_PIECE)
-            transpose_slab(0)
+            for slab in range(SLABS_BEFORE_SHIFT):
+                transpose_slab(slab)
+            centred = [head.tile([P, D], F32, name="centred%d" % m) for m in range(TOKEN_TILES)]
+            xn = [head.tile([P, D], BF16, name="xn%d" % m) for m in range(TOKEN_TILES)]
             pieces = [slice(j * CHUNK, (j + 1) * CHUNK) for j in range(D // CHUNK)]
-            centred = []
-            for m, (mean, op) in enumerate(((mean_var[:, 0:1], ALU.subtract), (minus_mean[:], ALU.add))):
-                centred.append(head.tile([P, D], F32, name="centred%d" % m))
-                for j, piece in enumerate(pieces):
+            for j, piece in enumerate(pieces):
+                for m in range(TOKEN_TILES):
                     nc.vector.scalar_tensor_tensor(
-                        out=centred[m][:, piece], in0=x_raw[m][:, piece], scalar=mean, in1=gain_banks[j][:],
-                        op0=op, op1=ALU.mult,
+                        out=centred[m][:, piece], in0=x_raw[m][:, piece], scalar=mean[m],
+                        in1=gain_banks[j][:], op0=ALU.subtract, op1=ALU.mult,
                     )
             shift_banks = spread_to_banks(SHIFT_PIECE)
-            xn = []
-            for m in range(TOKEN_TILES):
-                xn.append(head.tile([P, D], BF16, name="xn%d" % m))
-                for j, piece in enumerate(pieces):
-                    nc.vector.scalar_tensor_tensor(
-                        out=xn[m][:, piece], in0=centred[m][:, piece], scalar=rstds[m][:],
-                        in1=shift_banks[j][:], op0=ALU.mult, op1=ALU.add,
-                    )
-            for slab in range(1, SLABS_BEFORE_X):
+            for slab in range(SLABS_BEFORE_SHIFT, SLABS_BEFORE_X):
                 transpose_slab(slab)
-            spread_bias(0)
-            quantise_slab(0)
-            double_turns(64, HALF_E)
-            reduce_turns()
-
             grouped_x = head.tile([P, PASSES * TOKENS * PACK], BF16, align_bytes=64)
             dest_x = grouped_x[:].bitcast(F32).rearrange("p (g r u) -> p g r u", g=PASSES, u=2)
-            for g in range(PASSES):
-                transpose_words(lambda m: xn[m][:], g * WORDS_PER_PASS, TOKENS, dest_x[:, g, :, :])
+            for j, piece in enumerate(pieces):
+                for m in range(TOKEN_TILES):
+                    nc.vector.scalar_tensor_tensor(
+                        out=xn[m][:, piece], in0=centred[m][:, piece], scalar=rstd[m][:],
+                        in1=shift_banks[j][:], op0=ALU.mult, op1=ALU.add,
+                    )
+                transpose_words(
+                    lambda m, u: every_second_word(xn[m][:], j * WORDS_PER_PASS, u), TOKENS, dest_x[:, j, :, :]
+                )
+            for slab in range(QUANTISED_BEFORE_X):
+                quantise_slab(slab)
             nc.vector.quantize_mx(out=x_codes[:].bitcast(FP8X4), scales=x_scales[:], in_=grouped_x[:])
-
             for slab in range(SLABS_BEFORE_X, SLABS_AHEAD):
-                quantise_slab(slab - 1)
                 transpose_slab(slab)
+            for slab in range(QUANTISED_BEFORE_X, QUANTISE_AHEAD):
+                quantise_slab(slab)
 
         rot = pools.enter_context(tc.tile_pool(name="rot", bufs=4))
 
         def add_bias(c, m, dest):
-            nc.vector.tensor_tensor(out=dest, in0=acc[m][:], in1=bias_bc[c][:], op=ALU.add)
+            nc.vector.tensor_tensor(out=dest, in0=acc[c, m][:], in1=bias_bc[:, c * CHUNK : (c + 1) * CHUNK], op=ALU.add)
 
         def finish_v(c):
             cc = c - FIRST_V
@@ -358,21 +376,27 @@ def tile_rotaryembeddingtransformerlayer_pa_kernel(
                 for m, rows, rot_rows in pairs:
                     mix_queue.append((add_rotated, (which, m, rows, rot_rows, ready)))
 
+        def finish(c):
+            if c < FIRST_V:
+                finish_q_or_k(c)
+            else:
+                finish_v(c)
+
         def mix(steps):
             for step, args in mix_queue[:steps]:
                 step(*args)
             mix_queue[:] = mix_queue[steps:]
 
         def multiply(slab):
-            part = slab % SLABS_PER_CHUNK
+            c, part = divmod(slab, SLABS_PER_CHUNK)
             for i in range(SLAB_PASSES):
                 g = part * SLAB_PASSES + i
                 for m in range(TOKEN_TILES):
                     if g == 0:
-                        acc[m] = psum_acc.tile([P, CHUNK], F32, name="acc", tag="acc")
+                        acc[c, m] = psum_acc.tile([P, CHUNK], F32, name="acc", tag="acc")
                     tokens = slice(g * TOKENS + m * P, g * TOKENS + (m + 1) * P)
                     nc.tensor.matmul_mx(
-                        out=acc[m][:],
+                        out=acc[c, m][:],
                         lhsT=x_codes[:, tokens].bitcast(FP8X4),
                         lhsT_scale=x_scales[:, tokens],
                         rhs=w_codes[slab][:, i * CHUNK : (i + 1) * CHUNK].bitcast(FP8X4),
@@ -381,21 +405,16 @@ def tile_rotaryembeddingtransformerlayer_pa_kernel(
                         stop=(g == PASSES - 1),
                     )
 
-        for slab in range(SLABS_AHEAD, SLABS + SLABS_AHEAD):
-            multiply(slab - SLABS_AHEAD)
-            if slab % SLABS_PER_CHUNK == 0 and slab <= SLABS:
-                spread_bias(slab // SLABS_PER_CHUNK - 1)
-            if slab < SLABS:
-                transpose_slab(slab)
-            if slab - SLABS_AHEAD < len(table_steps):
-                step, args = table_steps[slab - SLABS_AHEAD]
+        for slab in range(SLABS):
+            multiply(slab)
+            if SLABS_AHEAD <= slab + AHEAD < SLABS:
+                transpose_slab(slab + AHEAD)
+            if slab + EARLY_TABLE_STEPS < len(table_steps):
+                step, args = table_steps[slab + EARLY_TABLE_STEPS]
                 step(*args)
-            if slab <= SLABS:
-                quantise_slab(slab - 1)
-            i, part = divmod(slab - SLABS_AHEAD, SLABS_PER_CHUNK)
-            if part == SLABS_PER_CHUNK - 1:
-                if ORDER[i] < FIRST_V:
-                    finish_q_or_k(ORDER[i])
-                else:
-                    finish_v(ORDER[i])
+            if slab > 0 and slab % SLABS_PER_CHUNK == 0:
+                finish(slab // SLABS_PER_CHUNK - 1)
             mix(MIX_STEPS)
+            if slab + QUANTISE_AHEAD < SLABS:
+                quantise_slab(slab + QUANTISE_AHEAD)
+        finish(CHUNKS - 1)

@@ -40,6 +40,7 @@ AHEAD = 3
 SLABS_BEFORE_SHIFT = 2
 SLABS_BEFORE_X = 4
 W_BUFS = 8
+BIAS_BEHIND = [0, 4, 12]
 SORTED = (1, 1)
 SORT_FROM = 6
 EARLY_TABLE_STEPS = 2
@@ -108,8 +109,8 @@ def tile_rotaryembeddingtransformerlayer_pa_kernel(
                     ].rearrange("(t p) k -> p t k", t=n),
                 )
 
-        def load_bias(c):
-            span = slice(c * CHUNK, (c + 1) * CHUNK)
+        def load_bias(which):
+            span = slice(which * E, (which + 1) * E)
             nc.sync.dma_start(out=bias_bc[:, span], in_=bqkv[span].partition_broadcast(P))
 
         def spread(piece, dest):
@@ -162,8 +163,8 @@ def tile_rotaryembeddingtransformerlayer_pa_kernel(
                     )
             if slab + W_BUFS < SLABS:
                 load_slab(slab + W_BUFS, 1)
-            if slab % SLABS_PER_CHUNK == 0:
-                load_bias(slab // SLABS_PER_CHUNK)
+            if slab in BIAS_BEHIND:
+                load_bias(BIAS_BEHIND.index(slab))
 
         def quantise_slab(slab):
             w_codes[slab] = code_pool.tile([P, SLAB_PASSES * CHUNK], U32, name="w_codes", align_bytes=64)

@@ -26,22 +26,20 @@ K_PASS = P * PACK
 PASSES = D // K_PASS
 WORDS_PER_PASS = K_PASS // 2
 
-CHUNK = 512
-ROW_TILES = CHUNK // P
-CHUNKS = 3 * E // CHUNK
-CHUNKS_PER_OUTPUT = E // CHUNK
-FIRST_V = 2 * CHUNKS_PER_OUTPUT
-SLAB_PASSES = 2
-SLAB_K = SLAB_PASSES * K_PASS
-SLABS_PER_CHUNK = PASSES // SLAB_PASSES
-SLABS = CHUNKS * SLABS_PER_CHUNK
+BANK = 512
+SLAB = 256
+ROW_TILES = SLAB // P
+SLABS = 3 * E // SLAB
+PAIRS_PER_OUTPUT = E // BANK
+FIRST_V = 2 * PAIRS_PER_OUTPUT
 SLABS_AHEAD = 6
 AHEAD = 3
 SLABS_BEFORE_SHIFT = 2
 SLABS_BEFORE_X = 4
 W_BUFS = 8
-BIAS_BEHIND = [0, 4, 12]
-SORTED = (1, 1)
+BIAS_PIECE = HALF_E
+FIRST_BIAS_LOAD, BIAS_LOAD_STEP = 6, 3
+SORTED = (1, 0)
 SORT_FROM = 6
 EARLY_TABLE_STEPS = 2
 MIX_STEPS = 2
@@ -98,20 +96,17 @@ def tile_rotaryembeddingtransformerlayer_pa_kernel(
         mix_queue = []
 
         def load_slab(slab, parts):
-            c, part = divmod(slab, SLABS_PER_CHUNK)
-            w_raw[slab] = w_pool.tile([P, ROW_TILES, SLAB_K], BF16, name="w_raw")
+            w_raw[slab] = w_pool.tile([P, ROW_TILES, D], BF16, name="w_raw")
+            rows = Wqkv[slab * SLAB : (slab + 1) * SLAB, :].rearrange("(p t) k -> p t k", t=ROW_TILES)
             n = ROW_TILES // parts
             for h in range(parts):
                 nc.sync.dma_start(
-                    out=w_raw[slab][:, h * n : (h + 1) * n, :],
-                    in_=Wqkv[
-                        c * CHUNK + h * n * P : c * CHUNK + (h + 1) * n * P, part * SLAB_K : (part + 1) * SLAB_K
-                    ].rearrange("(t p) k -> p t k", t=n),
+                    out=w_raw[slab][:, h * n : (h + 1) * n, :], in_=rows[:, h * n : (h + 1) * n, :]
                 )
-
-        def load_bias(which):
-            span = slice(which * E, (which + 1) * E)
-            nc.sync.dma_start(out=bias_bc[:, span], in_=bqkv[span].partition_broadcast(P))
+            since, rest = divmod(slab - FIRST_BIAS_LOAD, BIAS_LOAD_STEP)
+            if rest == 0 and 0 <= since < 3 * E // BIAS_PIECE:
+                span = slice(since * BIAS_PIECE, (since + 1) * BIAS_PIECE)
+                nc.sync.dma_start(out=bias_bc[:, span], in_=bqkv[span].partition_broadcast(P))
 
         def spread(piece, dest):
             nc.tensor.matmul(
@@ -119,56 +114,50 @@ def tile_rotaryembeddingtransformerlayer_pa_kernel(
                 start=True, stop=True,
             )
 
-        def every_second_word(row, w0, u):
-            return row.bitcast(F32)[:, w0 + u : w0 + WORDS_PER_PASS : 2]
+        def every_second_word(row, g, u):
+            return row.bitcast(F32)[:, g * WORDS_PER_PASS + u : (g + 1) * WORDS_PER_PASS : 2]
 
-        def transpose_words(words_of, width, dest_words):
-            w_t = psum_tr.tile([P, 2, width], F32, name="w_t", tag="tr")
-            for j in range(width // P):
+        def transpose_words(words_of, dest_words):
+            w_t = psum_tr.tile([P, 2, 2, P], F32, name="w_t", tag="tr")
+            for a in range(2):
                 for u in range(2):
-                    nc.tensor.transpose(w_t[:, u, j * P : (j + 1) * P], words_of(j, u), ident[:])
-            nc.scalar.copy(out=dest_words, in_=w_t[:].rearrange("p u n -> p n u"))
+                    nc.tensor.transpose(w_t[:, a, u, :], words_of(a, u), ident[:])
+            nc.scalar.copy(out=dest_words, in_=w_t[:].rearrange("p a u n -> p a n u"))
 
         def sort_slab(slab):
-            for g, tiles in enumerate(SORTED):
-                if tiles:
-                    w0 = g * WORDS_PER_PASS
-                    w_sorted[slab, g] = sorted_pool.tile([P, tiles, 2, P], F32, name="w_sorted%d" % g)
+            for t, pairs in enumerate(SORTED):
+                for h in range(pairs):
+                    w_sorted[slab, t, h] = sorted_pool.tile([P, 2, 2, P], F32, name="w_sorted%d%d" % (t, h))
                     nc.scalar.copy(
-                        out=w_sorted[slab, g][:],
-                        in_=w_raw[slab][:, 0:tiles, 2 * w0 : 2 * (w0 + WORDS_PER_PASS)].bitcast(F32).rearrange(
-                            "r t (p u) -> r t u p", u=2
+                        out=w_sorted[slab, t, h][:],
+                        in_=w_raw[slab][:, t, 2 * h * K_PASS : 2 * (h + 1) * K_PASS].bitcast(F32).rearrange(
+                            "r (g p u) -> r g u p", g=2, u=2
                         ),
                     )
 
         def transpose_slab(slab):
-            grouped[slab] = grouped_pool.tile(
-                [P, SLAB_PASSES * CHUNK * PACK], BF16, name="grouped", align_bytes=64
-            )
-            dest = grouped[slab][:].bitcast(F32).rearrange("p (g n u) -> p g n u", g=SLAB_PASSES, u=2)
+            grouped[slab] = grouped_pool.tile([P, SLAB * D // P], BF16, name="grouped", align_bytes=64)
+            dest = grouped[slab][:].bitcast(F32).rearrange("p (g n u) -> p g n u", g=PASSES, u=2)
 
-            def words_of(g, t, u):
-                if (slab, g) in w_sorted and t < SORTED[g]:
-                    return w_sorted[slab, g][:, t, u, :]
-                return every_second_word(w_raw[slab][:, t, :], g * WORDS_PER_PASS, u)
+            def words_of(t, h, a, u):
+                if (slab, t, h) in w_sorted:
+                    return w_sorted[slab, t, h][:, a, u, :]
+                return every_second_word(w_raw[slab][:, t, :], 2 * h + a, u)
 
             if SORT_FROM <= slab + 1 < SLABS:
                 sort_slab(slab + 1)
-            for g in range(SLAB_PASSES):
-                for h in range(2):
+            for t in range(ROW_TILES):
+                for h in range(PASSES // 2):
                     transpose_words(
-                        lambda j, u: words_of(g, 2 * h + j, u),
-                        2 * P,
-                        dest[:, g, h * 2 * P : (h + 1) * 2 * P, :],
+                        lambda a, u: words_of(t, h, a, u),
+                        dest[:, 2 * h : 2 * h + 2, t * P : (t + 1) * P, :],
                     )
             if slab + W_BUFS < SLABS:
                 load_slab(slab + W_BUFS, 1)
-            if slab in BIAS_BEHIND:
-                load_bias(BIAS_BEHIND.index(slab))
 
         def quantise_slab(slab):
-            w_codes[slab] = code_pool.tile([P, SLAB_PASSES * CHUNK], U32, name="w_codes", align_bytes=64)
-            w_scales[slab] = code_pool.tile([P, SLAB_PASSES * CHUNK], U8, name="w_scales", align_bytes=64)
+            w_codes[slab] = code_pool.tile([P, PASSES * SLAB], U32, name="w_codes", align_bytes=64)
+            w_scales[slab] = code_pool.tile([P, PASSES * SLAB], U8, name="w_scales", align_bytes=64)
             nc.vector.quantize_mx(
                 out=w_codes[slab][:].bitcast(FP8X4), scales=w_scales[slab][:], in_=grouped[slab][:]
             )
@@ -232,8 +221,8 @@ def tile_rotaryembeddingtransformerlayer_pa_kernel(
                 nc.sync.dma_start(
                     out=vectors[piece : piece + D // PIECE, :], in_=vector.rearrange("(r n) -> r n", n=PIECE)
                 )
+            load_slab(0, ROW_TILES)
             load_x(1)
-            load_slab(0, 2)
             for slab in range(1, W_BUFS):
                 load_slab(slab, 1)
 
@@ -282,10 +271,10 @@ def tile_rotaryembeddingtransformerlayer_pa_kernel(
 
             def spread_to_banks(first_piece):
                 banks = []
-                for j in range(D // CHUNK):
-                    bank = psum_acc.tile([P, CHUNK], F32, name="bank", tag="acc")
-                    for h in range(CHUNK // PIECE):
-                        spread(first_piece + j * (CHUNK // PIECE) + h, bank[:, h * PIECE : (h + 1) * PIECE])
+                for j in range(D // BANK):
+                    bank = psum_acc.tile([P, BANK], F32, name="bank", tag="acc")
+                    for h in range(BANK // PIECE):
+                        spread(first_piece + j * (BANK // PIECE) + h, bank[:, h * PIECE : (h + 1) * PIECE])
                     banks.append(bank)
                 return banks
 
@@ -296,7 +285,7 @@ def tile_rotaryembeddingtransformerlayer_pa_kernel(
                 transpose_slab(slab)
             centred = [head.tile([P, D], F32, name="centred%d" % m) for m in range(TOKEN_TILES)]
             xn = [head.tile([P, D], BF16, name="xn%d" % m) for m in range(TOKEN_TILES)]
-            pieces = [slice(j * CHUNK, (j + 1) * CHUNK) for j in range(D // CHUNK)]
+            pieces = [slice(j * BANK, (j + 1) * BANK) for j in range(D // BANK)]
             for j, piece in enumerate(pieces):
                 for m in range(TOKEN_TILES):
                     nc.vector.scalar_tensor_tensor(
@@ -307,16 +296,16 @@ def tile_rotaryembeddingtransformerlayer_pa_kernel(
             for slab in range(SLABS_BEFORE_SHIFT, SLABS_BEFORE_X):
                 transpose_slab(slab)
             grouped_x = head.tile([P, PASSES * TOKENS * PACK], BF16, align_bytes=64)
-            dest_x = grouped_x[:].bitcast(F32).rearrange("p (g r u) -> p g r u", g=PASSES, u=2)
+            dest_x = grouped_x[:].bitcast(F32).rearrange(
+                "p (g m n u) -> p g m n u", g=PASSES, m=TOKEN_TILES, u=2
+            )
             for j, piece in enumerate(pieces):
                 for m in range(TOKEN_TILES):
                     nc.vector.scalar_tensor_tensor(
                         out=xn[m][:, piece], in0=centred[m][:, piece], scalar=rstd[m][:],
                         in1=shift_banks[j][:], op0=ALU.mult, op1=ALU.add,
                     )
-                transpose_words(
-                    lambda m, u: every_second_word(xn[m][:], j * WORDS_PER_PASS, u), TOKENS, dest_x[:, j, :, :]
-                )
+                transpose_words(lambda m, u: every_second_word(xn[m][:], j, u), dest_x[:, j, :, :, :])
             for slab in range(QUANTISED_BEFORE_X):
                 quantise_slab(slab)
             nc.vector.quantize_mx(out=x_codes[:].bitcast(FP8X4), scales=x_scales[:], in_=grouped_x[:])
@@ -327,17 +316,21 @@ def tile_rotaryembeddingtransformerlayer_pa_kernel(
 
         rot = pools.enter_context(tc.tile_pool(name="rot", bufs=4))
 
-        def add_bias(c, m, dest):
-            nc.vector.tensor_tensor(out=dest, in0=acc[c, m][:], in1=bias_bc[:, c * CHUNK : (c + 1) * CHUNK], op=ALU.add)
+        def add_bias(pair, m, dest):
+            by_feature = dict(h=2, t=ROW_TILES)
+            nc.vector.tensor_tensor(
+                out=dest.rearrange("r (h p t) -> r h p t", **by_feature),
+                in0=acc[pair, m][:].rearrange("r (h t p) -> r h p t", **by_feature),
+                in1=bias_bc[:, pair * BANK : (pair + 1) * BANK].rearrange("r (h p t) -> r h p t", **by_feature),
+                op=ALU.add,
+            )
 
-        def finish_v(c):
-            cc = c - FIRST_V
+        def finish_v(pair):
+            columns = slice((pair - FIRST_V) * BANK, (pair - FIRST_V + 1) * BANK)
             for m in range(TOKEN_TILES):
-                v_rows = rot.tile([P, CHUNK], F32, name="v_rows")
-                add_bias(c, m, v_rows[:])
-                nc.sync.dma_start(
-                    out=out_rows[2][m * P : (m + 1) * P, cc * CHUNK : (cc + 1) * CHUNK], in_=v_rows[:]
-                )
+                v_rows = rot.tile([P, BANK], F32, name="v_rows")
+                add_bias(pair, m, v_rows[:])
+                nc.sync.dma_start(out=out_rows[2][m * P : (m + 1) * P, columns], in_=v_rows[:])
 
         def multiply_by_sin(rows, rot_rows, j):
             nc.vector.tensor_tensor(
@@ -359,16 +352,16 @@ def tile_rotaryembeddingtransformerlayer_pa_kernel(
             if span.stop == E:
                 nc.sync.dma_start(out=out_rows[which][m * P : (m + 1) * P, :], in_=rows[:])
 
-        def finish_q_or_k(c):
-            which, cc = divmod(c, CHUNKS_PER_OUTPUT)
+        def finish_q_or_k(pair):
+            which, s = divmod(pair, PAIRS_PER_OUTPUT)
             for m in range(TOKEN_TILES):
-                if cc == 0:
+                if s == 0:
                     q_rows[m] = rot.tile([P, E], F32, name="q_rows")
                     mixed[m] = rot.tile([P, E], F32, name="mixed", bufs=TOKEN_TILES)
-                add_bias(c, m, q_rows[m][:, cc * CHUNK : (cc + 1) * CHUNK])
-            if cc % 2 == 1:
-                j = cc // 2
-                ready = slice(0, CHUNK) if j == 0 else slice(CHUNK, E)
+                add_bias(pair, m, q_rows[m][:, s * BANK : (s + 1) * BANK])
+            if s % 2 == 1:
+                j = s // 2
+                ready = slice(0, HALF_E // 2) if j == 0 else slice(HALF_E // 2, E)
                 pairs = [(m, q_rows[m], mixed[m]) for m in range(TOKEN_TILES)]
                 for m, rows, rot_rows in pairs:
                     mix_queue.append((multiply_by_sin, (rows, rot_rows, j)))
@@ -377,11 +370,11 @@ def tile_rotaryembeddingtransformerlayer_pa_kernel(
                 for m, rows, rot_rows in pairs:
                     mix_queue.append((add_rotated, (which, m, rows, rot_rows, ready)))
 
-        def finish(c):
-            if c < FIRST_V:
-                finish_q_or_k(c)
+        def finish(pair):
+            if pair < FIRST_V:
+                finish_q_or_k(pair)
             else:
-                finish_v(c)
+                finish_v(pair)
 
         def mix(steps):
             for step, args in mix_queue[:steps]:
@@ -389,19 +382,20 @@ def tile_rotaryembeddingtransformerlayer_pa_kernel(
             mix_queue[:] = mix_queue[steps:]
 
         def multiply(slab):
-            c, part = divmod(slab, SLABS_PER_CHUNK)
-            for i in range(SLAB_PASSES):
-                g = part * SLAB_PASSES + i
+            pair, half = divmod(slab, 2)
+            columns = slice(half * SLAB, (half + 1) * SLAB)
+            for g in range(PASSES):
+                features = slice(g * SLAB, (g + 1) * SLAB)
                 for m in range(TOKEN_TILES):
-                    if g == 0:
-                        acc[c, m] = psum_acc.tile([P, CHUNK], F32, name="acc", tag="acc")
+                    if half == 0 and g == 0:
+                        acc[pair, m] = psum_acc.tile([P, BANK], F32, name="acc", tag="acc")
                     tokens = slice(g * TOKENS + m * P, g * TOKENS + (m + 1) * P)
                     nc.tensor.matmul_mx(
-                        out=acc[c, m][:],
+                        out=acc[pair, m][:, columns],
                         lhsT=x_codes[:, tokens].bitcast(FP8X4),
                         lhsT_scale=x_scales[:, tokens],
-                        rhs=w_codes[slab][:, i * CHUNK : (i + 1) * CHUNK].bitcast(FP8X4),
-                        rhs_scale=w_scales[slab][:, i * CHUNK : (i + 1) * CHUNK],
+                        rhs=w_codes[slab][:, features].bitcast(FP8X4),
+                        rhs_scale=w_scales[slab][:, features],
                         start=(g == 0),
                         stop=(g == PASSES - 1),
                     )
@@ -413,9 +407,9 @@ def tile_rotaryembeddingtransformerlayer_pa_kernel(
             if slab + EARLY_TABLE_STEPS < len(table_steps):
                 step, args = table_steps[slab + EARLY_TABLE_STEPS]
                 step(*args)
-            if slab > 0 and slab % SLABS_PER_CHUNK == 0:
-                finish(slab // SLABS_PER_CHUNK - 1)
+            if slab > 0 and slab % 2 == 0:
+                finish(slab // 2 - 1)
             mix(MIX_STEPS)
             if slab + QUANTISE_AHEAD < SLABS:
                 quantise_slab(slab + QUANTISE_AHEAD)
-        finish(CHUNKS - 1)
+        finish(SLABS // 2 - 1)

@@ -33,24 +33,23 @@ SLABS = 3 * E // SLAB
 PAIRS_PER_OUTPUT = E // BANK
 FIRST_V = 2 * PAIRS_PER_OUTPUT
 SLABS_AHEAD = 6
-AHEAD = 3
-SLABS_BEFORE_SHIFT = 2
+AHEAD = 4
 SLABS_BEFORE_X = 4
 W_BUFS = 8
-BIAS_PIECE = HALF_E
-FIRST_BIAS_LOAD, BIAS_LOAD_STEP = 6, 3
-SORTED = (1, 0)
+BIAS_AFTER = [4, 12]
+SORTED = (0, 0)
 SORT_FROM = 6
 EARLY_TABLE_STEPS = 2
 MIX_STEPS = 2
 GROUPED_BUFS = 6
 QUANTISE_AHEAD = 2
 CODE_BUFS = QUANTISE_AHEAD + 2
-QUANTISED_BEFORE_X = 2
+QUANTISED_BEFORE_X = 1
 
-PIECE = 256
-GAIN_PIECE, SHIFT_PIECE = 0, D // PIECE
-PIECES = 2 * D // PIECE
+PIECE = 512
+GAIN_PIECE, SHIFT_PIECE, BIAS_PIECE = 0, D // PIECE, 2 * D // PIECE
+PIECES = (2 * D + 3 * E) // PIECE
+HALF_D = D // 2
 
 ROUND = 1.5 * 2.0**23
 FREQ_RATIO = 10000.0 ** (-1.0 / HALF_E)
@@ -103,16 +102,24 @@ def tile_rotaryembeddingtransformerlayer_pa_kernel(
                 nc.sync.dma_start(
                     out=w_raw[slab][:, h * n : (h + 1) * n, :], in_=rows[:, h * n : (h + 1) * n, :]
                 )
-            since, rest = divmod(slab - FIRST_BIAS_LOAD, BIAS_LOAD_STEP)
-            if rest == 0 and 0 <= since < 3 * E // BIAS_PIECE:
-                span = slice(since * BIAS_PIECE, (since + 1) * BIAS_PIECE)
-                nc.sync.dma_start(out=bias_bc[:, span], in_=bqkv[span].partition_broadcast(P))
 
         def spread(piece, dest):
             nc.tensor.matmul(
                 dest, lhsT=select[:, piece : piece + 1].to_broadcast([P, P]), rhs=vectors[:],
                 start=True, stop=True,
             )
+
+        def spread_half(piece, pool, tag):
+            bank = pool.tile([P, HALF_D], BF16, name="bank", tag=tag)
+            for i in range(HALF_D // PIECE):
+                spread(piece + i, bank[:, i * PIECE : (i + 1) * PIECE])
+            return bank
+
+        def spread_bias(which):
+            for j in range(E // HALF_D):
+                first = which * E + j * HALF_D
+                bank = spread_half(BIAS_PIECE + first // PIECE, psum_tr, "tr")
+                nc.scalar.copy(out=bias_bc[:, first : first + HALF_D], in_=bank[:])
 
         def every_second_word(row, g, u):
             return row.bitcast(F32)[:, g * WORDS_PER_PASS + u : (g + 1) * WORDS_PER_PASS : 2]
@@ -135,7 +142,7 @@ def tile_rotaryembeddingtransformerlayer_pa_kernel(
                         ),
                     )
 
-        def transpose_slab(slab):
+        def transpose_slab(slab, between=None):
             grouped[slab] = grouped_pool.tile([P, SLAB * D // P], BF16, name="grouped", align_bytes=64)
             dest = grouped[slab][:].bitcast(F32).rearrange("p (g n u) -> p g n u", g=PASSES, u=2)
 
@@ -146,21 +153,27 @@ def tile_rotaryembeddingtransformerlayer_pa_kernel(
 
             if SORT_FROM <= slab + 1 < SLABS:
                 sort_slab(slab + 1)
-            for t in range(ROW_TILES):
-                for h in range(PASSES // 2):
-                    transpose_words(
-                        lambda a, u: words_of(t, h, a, u),
-                        dest[:, 2 * h : 2 * h + 2, t * P : (t + 1) * P, :],
-                    )
+            order = [(h, t) for h in range(PASSES // 2) for t in range(ROW_TILES)]
+            for h, t in order:
+                transpose_words(
+                    lambda a, u: words_of(t, h, a, u), dest[:, 2 * h : 2 * h + 2, t * P : (t + 1) * P, :]
+                )
+                if (h, t) == order[1] and between is not None:
+                    between()
             if slab + W_BUFS < SLABS:
                 load_slab(slab + W_BUFS, 1)
 
-        def quantise_slab(slab):
+        def quantise_slab(slab, parts=1):
             w_codes[slab] = code_pool.tile([P, PASSES * SLAB], U32, name="w_codes", align_bytes=64)
             w_scales[slab] = code_pool.tile([P, PASSES * SLAB], U8, name="w_scales", align_bytes=64)
-            nc.vector.quantize_mx(
-                out=w_codes[slab][:].bitcast(FP8X4), scales=w_scales[slab][:], in_=grouped[slab][:]
-            )
+            n = PASSES * SLAB // parts
+            for i in range(parts):
+                words = slice(i * n, (i + 1) * n)
+                nc.vector.quantize_mx(
+                    out=w_codes[slab][:, words].bitcast(FP8X4),
+                    scales=w_scales[slab][:, words],
+                    in_=grouped[slab][:, i * n * PACK : (i + 1) * n * PACK],
+                )
 
         turns = sin_t[:, 0:HALF_E]
         abs_turns = sin_t[:, HALF_E : HALF_E + REDUCED]
@@ -217,9 +230,9 @@ def tile_rotaryembeddingtransformerlayer_pa_kernel(
             def load_x(m):
                 nc.sync.dma_start(out=x_raw[m][:], in_=x_rows[m * P : (m + 1) * P, :])
             load_x(0)
-            for piece, vector in ((GAIN_PIECE, g1), (SHIFT_PIECE, be1)):
+            for piece, vector in ((GAIN_PIECE, g1), (SHIFT_PIECE, be1), (BIAS_PIECE, bqkv)):
                 nc.sync.dma_start(
-                    out=vectors[piece : piece + D // PIECE, :], in_=vector.rearrange("(r n) -> r n", n=PIECE)
+                    out=vectors[piece : piece + vector.shape[0] // PIECE, :], in_=vector.rearrange("(r n) -> r n", n=PIECE)
                 )
             load_slab(0, ROW_TILES)
             load_x(1)
@@ -244,9 +257,10 @@ def tile_rotaryembeddingtransformerlayer_pa_kernel(
             nc.gpsimd.memset(minus_half[:], -0.5)
             table_load = head.tile([P, 1], F32)
             nc.scalar.activation(out=table_load[:], in_=pos[:], func=ACT.Sin, scale=1.0 / POSITIONS)
-            double_turns(1, HALF_E)
-            reduce_turns()
+            double_turns(1, 256)
             nc.vector.tensor_copy(out=select[:], in_=ident[:, 0:PIECES])
+            double_turns(256, HALF_E)
+            reduce_turns()
             for step, args in table_steps[:EARLY_TABLE_STEPS]:
                 step(*args)
 
@@ -269,47 +283,43 @@ def tile_rotaryembeddingtransformerlayer_pa_kernel(
                 mean.append(mean_var[:, 0:1])
                 take_rstd(m, mean_var[:, 1:2])
 
-            def spread_to_banks(first_piece):
-                banks = []
-                for j in range(D // BANK):
-                    bank = psum_acc.tile([P, BANK], F32, name="bank", tag="acc")
-                    for h in range(BANK // PIECE):
-                        spread(first_piece + j * (BANK // PIECE) + h, bank[:, h * PIECE : (h + 1) * PIECE])
-                    banks.append(bank)
-                return banks
-
+            gain_banks = [spread_half(GAIN_PIECE + j * HALF_D // PIECE, psum_acc, "acc") for j in range(2)]
+            shift_banks = [spread_half(SHIFT_PIECE + j * HALF_D // PIECE, psum_acc, "acc") for j in range(2)]
+            spread_bias(0)
             for m in range(TOKEN_TILES):
                 take_stats(m)
-            gain_banks = spread_to_banks(GAIN_PIECE)
-            for slab in range(SLABS_BEFORE_SHIFT):
+            for slab in range(SLABS_BEFORE_X):
                 transpose_slab(slab)
             centred = [head.tile([P, D], F32, name="centred%d" % m) for m in range(TOKEN_TILES)]
             xn = [head.tile([P, D], BF16, name="xn%d" % m) for m in range(TOKEN_TILES)]
-            pieces = [slice(j * BANK, (j + 1) * BANK) for j in range(D // BANK)]
-            for j, piece in enumerate(pieces):
-                for m in range(TOKEN_TILES):
-                    nc.vector.scalar_tensor_tensor(
-                        out=centred[m][:, piece], in0=x_raw[m][:, piece], scalar=mean[m],
-                        in1=gain_banks[j][:], op0=ALU.subtract, op1=ALU.mult,
-                    )
-            shift_banks = spread_to_banks(SHIFT_PIECE)
-            for slab in range(SLABS_BEFORE_SHIFT, SLABS_BEFORE_X):
-                transpose_slab(slab)
             grouped_x = head.tile([P, PASSES * TOKENS * PACK], BF16, align_bytes=64)
             dest_x = grouped_x[:].bitcast(F32).rearrange(
                 "p (g m n u) -> p g m n u", g=PASSES, m=TOKEN_TILES, u=2
             )
-            for j, piece in enumerate(pieces):
+            halves = [slice(0, HALF_D), slice(HALF_D, D)]
+            for j, half in enumerate(halves):
                 for m in range(TOKEN_TILES):
                     nc.vector.scalar_tensor_tensor(
-                        out=xn[m][:, piece], in0=centred[m][:, piece], scalar=rstd[m][:],
+                        out=centred[m][:, half], in0=x_raw[m][:, half], scalar=mean[m],
+                        in1=gain_banks[j][:], op0=ALU.subtract, op1=ALU.mult,
+                    )
+            for j, half in enumerate(halves):
+                for m in range(TOKEN_TILES):
+                    nc.vector.scalar_tensor_tensor(
+                        out=xn[m][:, half], in0=centred[m][:, half], scalar=rstd[m][:],
                         in1=shift_banks[j][:], op0=ALU.mult, op1=ALU.add,
                     )
-                transpose_words(lambda m, u: every_second_word(xn[m][:], j, u), dest_x[:, j, :, :, :])
+
+            def transpose_x(j):
+                for g in range(j * PASSES // 2, (j + 1) * PASSES // 2):
+                    transpose_words(lambda m, u: every_second_word(xn[m][:], g, u), dest_x[:, g, :, :, :])
+
+            transpose_x(0)
+            transpose_slab(SLABS_BEFORE_X, between=lambda: transpose_x(1))
             for slab in range(QUANTISED_BEFORE_X):
                 quantise_slab(slab)
             nc.vector.quantize_mx(out=x_codes[:].bitcast(FP8X4), scales=x_scales[:], in_=grouped_x[:])
-            for slab in range(SLABS_BEFORE_X, SLABS_AHEAD):
+            for slab in range(SLABS_BEFORE_X + 1, SLABS_AHEAD):
                 transpose_slab(slab)
             for slab in range(QUANTISED_BEFORE_X, QUANTISE_AHEAD):
                 quantise_slab(slab)
@@ -402,6 +412,8 @@ def tile_rotaryembeddingtransformerlayer_pa_kernel(
 
         for slab in range(SLABS):
             multiply(slab)
+            if slab in BIAS_AFTER:
+                spread_bias(1 + BIAS_AFTER.index(slab))
             if SLABS_AHEAD <= slab + AHEAD < SLABS:
                 transpose_slab(slab + AHEAD)
             if slab + EARLY_TABLE_STEPS < len(table_steps):
@@ -411,5 +423,5 @@ def tile_rotaryembeddingtransformerlayer_pa_kernel(
                 finish(slab // 2 - 1)
             mix(MIX_STEPS)
             if slab + QUANTISE_AHEAD < SLABS:
-                quantise_slab(slab + QUANTISE_AHEAD)
+                quantise_slab(slab + QUANTISE_AHEAD, 2 if slab + QUANTISE_AHEAD == SLABS - 1 else 1)
         finish(SLABS // 2 - 1)

@@ -36,9 +36,10 @@ SLABS_AHEAD = 6
 AHEAD = 4
 SLABS_BEFORE_X = 4
 W_BUFS = 8
-BIAS_AFTER = [4, 12]
-SORTED = (0, 0)
-SORT_FROM = 6
+BIAS_AFTER = [0, 7, 14]
+SORTED = (1, 0)
+SORT_FROM = 8
+SORT_AHEAD = 2
 EARLY_TABLE_STEPS = 2
 MIX_STEPS = 2
 GROUPED_BUFS = 6
@@ -70,7 +71,7 @@ def tile_rotaryembeddingtransformerlayer_pa_kernel(
         const = pools.enter_context(tc.tile_pool(name="const", bufs=1))
         w_pool = pools.enter_context(tc.tile_pool(name="w_raw", bufs=W_BUFS))
         grouped_pool = pools.enter_context(tc.tile_pool(name="grouped", bufs=GROUPED_BUFS))
-        sorted_pool = pools.enter_context(tc.tile_pool(name="sorted", bufs=2))
+        sorted_pool = pools.enter_context(tc.tile_pool(name="sorted", bufs=SORT_AHEAD + 1))
         code_pool = pools.enter_context(tc.tile_pool(name="codes", bufs=CODE_BUFS))
         psum_tr = pools.enter_context(tc.psum_pool(name="psum_tr", bufs=4))
         psum_acc = pools.enter_context(tc.psum_pool(name="psum_acc", bufs=4))
@@ -151,8 +152,6 @@ def tile_rotaryembeddingtransformerlayer_pa_kernel(
                     return w_sorted[slab, t, h][:, a, u, :]
                 return every_second_word(w_raw[slab][:, t, :], 2 * h + a, u)
 
-            if SORT_FROM <= slab + 1 < SLABS:
-                sort_slab(slab + 1)
             order = [(h, t) for h in range(PASSES // 2) for t in range(ROW_TILES)]
             for h, t in order:
                 transpose_words(
@@ -160,6 +159,8 @@ def tile_rotaryembeddingtransformerlayer_pa_kernel(
                 )
                 if (h, t) == order[1] and between is not None:
                     between()
+            if SORT_FROM <= slab + SORT_AHEAD < SLABS:
+                sort_slab(slab + SORT_AHEAD)
             if slab + W_BUFS < SLABS:
                 load_slab(slab + W_BUFS, 1)
 
@@ -231,7 +232,7 @@ def tile_rotaryembeddingtransformerlayer_pa_kernel(
                 nc.sync.dma_start(out=x_raw[m][:], in_=x_rows[m * P : (m + 1) * P, :])
             load_x(0)
             for piece, vector in ((GAIN_PIECE, g1), (SHIFT_PIECE, be1), (BIAS_PIECE, bqkv)):
-                nc.sync.dma_start(
+                nc.scalar.dma_start(
                     out=vectors[piece : piece + vector.shape[0] // PIECE, :], in_=vector.rearrange("(r n) -> r n", n=PIECE)
                 )
             load_slab(0, ROW_TILES)
@@ -285,7 +286,6 @@ def tile_rotaryembeddingtransformerlayer_pa_kernel(
 
             gain_banks = [spread_half(GAIN_PIECE + j * HALF_D // PIECE, psum_acc, "acc") for j in range(2)]
             shift_banks = [spread_half(SHIFT_PIECE + j * HALF_D // PIECE, psum_acc, "acc") for j in range(2)]
-            spread_bias(0)
             for m in range(TOKEN_TILES):
                 take_stats(m)
             for slab in range(SLABS_BEFORE_X):
@@ -326,21 +326,26 @@ def tile_rotaryembeddingtransformerlayer_pa_kernel(
 
         rot = pools.enter_context(tc.tile_pool(name="rot", bufs=4))
 
-        def add_bias(pair, m, dest):
-            by_feature = dict(h=2, t=ROW_TILES)
+        def add_bias(pair, m, dest, first=0, slabs=2):
+            by_feature = dict(h=slabs, t=ROW_TILES)
+            columns = slice(first * SLAB, (first + slabs) * SLAB)
+            features = slice((2 * pair + first) * SLAB, (2 * pair + first + slabs) * SLAB)
             nc.vector.tensor_tensor(
                 out=dest.rearrange("r (h p t) -> r h p t", **by_feature),
-                in0=acc[pair, m][:].rearrange("r (h t p) -> r h p t", **by_feature),
-                in1=bias_bc[:, pair * BANK : (pair + 1) * BANK].rearrange("r (h p t) -> r h p t", **by_feature),
+                in0=acc[pair, m][:, columns].rearrange("r (h t p) -> r h p t", **by_feature),
+                in1=bias_bc[:, features].rearrange("r (h p t) -> r h p t", **by_feature),
                 op=ALU.add,
             )
 
-        def finish_v(pair):
-            columns = slice((pair - FIRST_V) * BANK, (pair - FIRST_V + 1) * BANK)
+        def finish_v(pair, first=0, slabs=2):
+            start = (2 * (pair - FIRST_V) + first) * SLAB
             for m in range(TOKEN_TILES):
-                v_rows = rot.tile([P, BANK], F32, name="v_rows")
-                add_bias(pair, m, v_rows[:])
-                nc.sync.dma_start(out=out_rows[2][m * P : (m + 1) * P, columns], in_=v_rows[:])
+                v_rows = rot.tile([P, BANK], F32, name="v_rows", bufs=6)
+                add_bias(pair, m, v_rows[:, 0 : slabs * SLAB], first, slabs)
+                nc.sync.dma_start(
+                    out=out_rows[2][m * P : (m + 1) * P, start : start + slabs * SLAB],
+                    in_=v_rows[:, 0 : slabs * SLAB],
+                )
 
         def multiply_by_sin(rows, rot_rows, j):
             nc.vector.tensor_tensor(
@@ -413,7 +418,7 @@ def tile_rotaryembeddingtransformerlayer_pa_kernel(
         for slab in range(SLABS):
             multiply(slab)
             if slab in BIAS_AFTER:
-                spread_bias(1 + BIAS_AFTER.index(slab))
+                spread_bias(BIAS_AFTER.index(slab))
             if SLABS_AHEAD <= slab + AHEAD < SLABS:
                 transpose_slab(slab + AHEAD)
             if slab + EARLY_TABLE_STEPS < len(table_steps):
@@ -421,7 +426,9 @@ def tile_rotaryembeddingtransformerlayer_pa_kernel(
                 step(*args)
             if slab > 0 and slab % 2 == 0:
                 finish(slab // 2 - 1)
+            if slab == SLABS - 1:
+                finish_v(SLABS // 2 - 1, first=0, slabs=1)
             mix(MIX_STEPS)
             if slab + QUANTISE_AHEAD < SLABS:
                 quantise_slab(slab + QUANTISE_AHEAD, 2 if slab + QUANTISE_AHEAD == SLABS - 1 else 1)
-        finish(SLABS // 2 - 1)
+        finish_v(SLABS // 2 - 1, first=1, slabs=1)

@@ -33,19 +33,19 @@ SLABS = 3 * E // SLAB
 PAIRS_PER_OUTPUT = E // BANK
 FIRST_V = 2 * PAIRS_PER_OUTPUT
 SLABS_AHEAD = 6
-AHEAD = 4
+AHEAD = 3
 SLABS_BEFORE_X = 4
 W_BUFS = 8
 BIAS_AFTER = [0, 7, 14]
 SORTED = (1, 0)
-SORT_FROM = 8
+SORT_FROM = 12
 SORT_AHEAD = 2
-EARLY_TABLE_STEPS = 2
-MIX_STEPS = 2
+EARLY_TABLE_STEPS = 1
+MIX_STEPS = 1
 GROUPED_BUFS = 6
 QUANTISE_AHEAD = 2
 CODE_BUFS = QUANTISE_AHEAD + 2
-QUANTISED_BEFORE_X = 1
+QUANTISED_BEFORE_X = 2
 
 PIECE = 512
 GAIN_PIECE, SHIFT_PIECE, BIAS_PIECE = 0, D // PIECE, 2 * D // PIECE
@@ -191,10 +191,11 @@ def tile_rotaryembeddingtransformerlayer_pa_kernel(
 
         def reduce_turns():
             low = turns[:, 0:REDUCED]
-            nc.vector.tensor_scalar(
-                out=whole, in0=low, scalar1=ROUND, scalar2=ROUND, op0=ALU.add, op1=ALU.subtract
-            )
-            nc.vector.tensor_tensor(out=low, in0=low, in1=whole, op=ALU.subtract)
+            for source, shift in ((low, ROUND), (whole, -ROUND)):
+                nc.gpsimd.tensor_scalar(
+                    out=whole, in0=source, scalar1=1.0, scalar2=shift, op0=ALU.mult, op1=ALU.add
+                )
+            nc.gpsimd.tensor_tensor(out=low, in0=low, in1=whole, op=ALU.subtract)
 
         def fill_emb_sin():
             nc.scalar.activation(out=cos_t[:, 0:HALF_E], in_=turns, func=ACT.Sin, scale=2.0 * math.pi)
@@ -232,7 +233,7 @@ def tile_rotaryembeddingtransformerlayer_pa_kernel(
                 nc.sync.dma_start(out=x_raw[m][:], in_=x_rows[m * P : (m + 1) * P, :])
             load_x(0)
             for piece, vector in ((GAIN_PIECE, g1), (SHIFT_PIECE, be1), (BIAS_PIECE, bqkv)):
-                nc.scalar.dma_start(
+                nc.sync.dma_start(
                     out=vectors[piece : piece + vector.shape[0] // PIECE, :], in_=vector.rearrange("(r n) -> r n", n=PIECE)
                 )
             load_slab(0, ROW_TILES)
@@ -347,43 +348,45 @@ def tile_rotaryembeddingtransformerlayer_pa_kernel(
                     in_=v_rows[:, 0 : slabs * SLAB],
                 )
 
+        def for_both_tiles(table):
+            return table.unsqueeze(1).broadcast_to([P, TOKEN_TILES] + list(table.shape[1:]))
+
         def multiply_by_sin(rows, rot_rows, j):
             nc.vector.tensor_tensor(
-                out=rot_rows[:].rearrange("r (h j i) -> r h j i", h=2, j=2)[:, :, j, :],
-                in0=rows[:, j * HALF_E : (j + 1) * HALF_E].rearrange("r (i h) -> r h i", h=2),
-                in1=sin_t[:].rearrange("r (h j i) -> r h j i", h=2, j=2)[:, :, j, :],
+                out=rot_rows[:].rearrange("r m (h j i) -> r m h j i", h=2, j=2)[:, :, :, j, :],
+                in0=rows[:, :, j * HALF_E : (j + 1) * HALF_E].rearrange("r m (i h) -> r m h i", h=2),
+                in1=for_both_tiles(sin_t[:].rearrange("r (h j i) -> r h j i", h=2, j=2)[:, :, j, :]),
                 op=ALU.mult,
             )
 
         def multiply_by_cos(rows, j):
             span = slice(j * HALF_E, (j + 1) * HALF_E)
-            nc.vector.tensor_tensor(out=rows[:, span], in0=rows[:, span], in1=cos_t[:, span], op=ALU.mult)
-
-        def add_rotated(which, m, rows, rot_rows, span):
             nc.vector.tensor_tensor(
-                out=rows[:, span], in0=rows[:, span], in1=rot_rows[:, span],
+                out=rows[:, :, span], in0=rows[:, :, span], in1=for_both_tiles(cos_t[:, span]), op=ALU.mult
+            )
+
+        def add_rotated(which, rows, rot_rows, span):
+            nc.vector.tensor_tensor(
+                out=rows[:, :, span], in0=rows[:, :, span], in1=rot_rows[:, :, span],
                 op=(ALU.add if which == 0 else ALU.subtract),
             )
             if span.stop == E:
-                nc.sync.dma_start(out=out_rows[which][m * P : (m + 1) * P, :], in_=rows[:])
+                for m in range(TOKEN_TILES):
+                    nc.sync.dma_start(out=out_rows[which][m * P : (m + 1) * P, :], in_=rows[:, m, :])
 
         def finish_q_or_k(pair):
             which, s = divmod(pair, PAIRS_PER_OUTPUT)
+            if s == 0:
+                q_rows[which] = rot.tile([P, TOKEN_TILES, E], F32, name="q_rows", bufs=2)
+                mixed[which] = rot.tile([P, TOKEN_TILES, E], F32, name="mixed", bufs=1)
             for m in range(TOKEN_TILES):
-                if s == 0:
-                    q_rows[m] = rot.tile([P, E], F32, name="q_rows")
-                    mixed[m] = rot.tile([P, E], F32, name="mixed", bufs=TOKEN_TILES)
-                add_bias(pair, m, q_rows[m][:, s * BANK : (s + 1) * BANK])
+                add_bias(pair, m, q_rows[which][:, m, s * BANK : (s + 1) * BANK])
             if s % 2 == 1:
                 j = s // 2
                 ready = slice(0, HALF_E // 2) if j == 0 else slice(HALF_E // 2, E)
-                pairs = [(m, q_rows[m], mixed[m]) for m in range(TOKEN_TILES)]
-                for m, rows, rot_rows in pairs:
-                    mix_queue.append((multiply_by_sin, (rows, rot_rows, j)))
-                for m, rows, rot_rows in pairs:
-                    mix_queue.append((multiply_by_cos, (rows, j)))
-                for m, rows, rot_rows in pairs:
-                    mix_queue.append((add_rotated, (which, m, rows, rot_rows, ready)))
+                mix_queue.append((multiply_by_sin, (q_rows[which], mixed[which], j)))
+                mix_queue.append((multiply_by_cos, (q_rows[which], j)))
+                mix_queue.append((add_rotated, (which, q_rows[which], mixed[which], ready)))
 
         def finish(pair):
             if pair < FIRST_V:

import math
from contextlib import ExitStack

import concourse.mybir as mybir
from concourse.masks import make_identity

F32 = mybir.dt.float32
BF16 = mybir.dt.bfloat16
U32 = mybir.dt.uint32
U8 = mybir.dt.uint8
FP8X4 = mybir.dt.float8_e4m3fn_x4
ALU = mybir.AluOpType
ACT = mybir.ActivationFunctionType

P = 128
TOKENS = 256
POSITIONS = 64
TOKEN_TILES = TOKENS // P
D = 2048
E = 2048
HALF_E = E // 2
EPS = 1e-5

PACK = 4
K_PASS = P * PACK
PASSES = D // K_PASS
WORDS_PER_PASS = K_PASS // 2

BANK = 512
SLAB = 256
ROW_TILES = SLAB // P
SLABS = 3 * E // SLAB
PAIRS_PER_OUTPUT = E // BANK
FIRST_V = 2 * PAIRS_PER_OUTPUT
SLABS_AHEAD = 6
AHEAD = 3
SLABS_BEFORE_X = 4
W_BUFS = 8
BIAS_AFTER = [0, 7, 14]
SORTED = (1, 0)
SORT_FROM = 12
SORT_AHEAD = 2
EARLY_TABLE_STEPS = 1
MIX_STEPS = 1
GROUPED_BUFS = 6
QUANTISE_AHEAD = 2
CODE_BUFS = QUANTISE_AHEAD + 2
QUANTISED_BEFORE_X = 2

PIECE = 512
GAIN_PIECE, SHIFT_PIECE, BIAS_PIECE = 0, D // PIECE, 2 * D // PIECE
PIECES = (2 * D + 3 * E) // PIECE
HALF_D = D // 2

ROUND = 1.5 * 2.0**23
FREQ_RATIO = 10000.0 ** (-1.0 / HALF_E)
REDUCED = HALF_E // 2

FLOPS = 2 * TOKENS * D * 3 * E


def tile_rotaryembeddingtransformerlayer_pa_kernel(
    tc, src, Wqkv, bqkv, g1, be1, out_q, out_k, out_v
):
    nc = tc.nc
    x_rows = src.flatten_outer_dims()
    out_rows = [out_q.flatten_outer_dims(), out_k.flatten_outer_dims(), out_v.flatten_outer_dims()]

    with ExitStack() as pools:
        pools.enter_context(tc.manual_schedule())
        const = pools.enter_context(tc.tile_pool(name="const", bufs=1))
        w_pool = pools.enter_context(tc.tile_pool(name="w_raw", bufs=W_BUFS))
        grouped_pool = pools.enter_context(tc.tile_pool(name="grouped", bufs=GROUPED_BUFS))
        sorted_pool = pools.enter_context(tc.tile_pool(name="sorted", bufs=SORT_AHEAD + 1))
        code_pool = pools.enter_context(tc.tile_pool(name="codes", bufs=CODE_BUFS))
        psum_tr = pools.enter_context(tc.psum_pool(name="psum_tr", bufs=4))
        psum_acc = pools.enter_context(tc.psum_pool(name="psum_acc", bufs=4))

        ident = const.tile([P, P], F32)
        vectors = const.tile([P, PIECE], BF16)
        bias_bc = const.tile([P, 3 * E], BF16)
        select = const.tile([P, PIECES], BF16)
        x_codes = const.tile([P, PASSES * TOKENS], U32, align_bytes=64)
        x_scales = const.tile([P, PASSES * TOKENS], U8, align_bytes=64)
        cos_t = const.tile([P, E], F32)
        sin_t = const.tile([P, E], F32)

        w_raw = {}
        w_sorted = {}
        grouped = {}
        w_codes = {}
        w_scales = {}
        acc = {}
        q_rows = {}
        mixed = {}
        mix_queue = []

        def load_slab(slab, parts):
            w_raw[slab] = w_pool.tile([P, ROW_TILES, D], BF16, name="w_raw")
            rows = Wqkv[slab * SLAB : (slab + 1) * SLAB, :].rearrange("(p t) k -> p t k", t=ROW_TILES)
            n = ROW_TILES // parts
            for h in range(parts):
                nc.sync.dma_start(
                    out=w_raw[slab][:, h * n : (h + 1) * n, :], in_=rows[:, h * n : (h + 1) * n, :]
                )

        def spread(piece, dest):
            nc.tensor.matmul(
                dest, lhsT=select[:, piece : piece + 1].to_broadcast([P, P]), rhs=vectors[:],
                start=True, stop=True,
            )

        def spread_half(piece, pool, tag):
            bank = pool.tile([P, HALF_D], BF16, name="bank", tag=tag)
            for i in range(HALF_D // PIECE):
                spread(piece + i, bank[:, i * PIECE : (i + 1) * PIECE])
            return bank

        def spread_bias(which):
            for j in range(E // HALF_D):
                first = which * E + j * HALF_D
                bank = spread_half(BIAS_PIECE + first // PIECE, psum_tr, "tr")
                nc.scalar.copy(out=bias_bc[:, first : first + HALF_D], in_=bank[:])

        def every_second_word(row, g, u):
            return row.bitcast(F32)[:, g * WORDS_PER_PASS + u : (g + 1) * WORDS_PER_PASS : 2]

        def transpose_words(words_of, dest_words):
            w_t = psum_tr.tile([P, 2, 2, P], F32, name="w_t", tag="tr")
            for a in range(2):
                for u in range(2):
                    nc.tensor.transpose(w_t[:, a, u, :], words_of(a, u), ident[:])
            nc.scalar.copy(out=dest_words, in_=w_t[:].rearrange("p a u n -> p a n u"))

        def sort_slab(slab):
            for t, pairs in enumerate(SORTED):
                for h in range(pairs):
                    w_sorted[slab, t, h] = sorted_pool.tile([P, 2, 2, P], F32, name="w_sorted%d%d" % (t, h))
                    nc.scalar.copy(
                        out=w_sorted[slab, t, h][:],
                        in_=w_raw[slab][:, t, 2 * h * K_PASS : 2 * (h + 1) * K_PASS].bitcast(F32).rearrange(
                            "r (g p u) -> r g u p", g=2, u=2
                        ),
                    )

        def transpose_slab(slab, between=None):
            grouped[slab] = grouped_pool.tile([P, SLAB * D // P], BF16, name="grouped", align_bytes=64)
            dest = grouped[slab][:].bitcast(F32).rearrange("p (g n u) -> p g n u", g=PASSES, u=2)

            def words_of(t, h, a, u):
                if (slab, t, h) in w_sorted:
                    return w_sorted[slab, t, h][:, a, u, :]
                return every_second_word(w_raw[slab][:, t, :], 2 * h + a, u)

            order = [(h, t) for h in range(PASSES // 2) for t in range(ROW_TILES)]
            for h, t in order:
                transpose_words(
                    lambda a, u: words_of(t, h, a, u), dest[:, 2 * h : 2 * h + 2, t * P : (t + 1) * P, :]
                )
                if (h, t) == order[1] and between is not None:
                    between()
            if SORT_FROM <= slab + SORT_AHEAD < SLABS:
                sort_slab(slab + SORT_AHEAD)
            if slab + W_BUFS < SLABS:
                load_slab(slab + W_BUFS, 1)

        def quantise_slab(slab, parts=1):
            w_codes[slab] = code_pool.tile([P, PASSES * SLAB], U32, name="w_codes", align_bytes=64)
            w_scales[slab] = code_pool.tile([P, PASSES * SLAB], U8, name="w_scales", align_bytes=64)
            n = PASSES * SLAB // parts
            for i in range(parts):
                words = slice(i * n, (i + 1) * n)
                nc.vector.quantize_mx(
                    out=w_codes[slab][:, words].bitcast(FP8X4),
                    scales=w_scales[slab][:, words],
                    in_=grouped[slab][:, i * n * PACK : (i + 1) * n * PACK],
                )

        turns = sin_t[:, 0:HALF_E]
        abs_turns = sin_t[:, HALF_E : HALF_E + REDUCED]
        whole = sin_t[:, HALF_E + REDUCED : E]

        def double_turns(first, last):
            n = first
            while n < last:
                nc.vector.tensor_scalar(
                    out=turns[:, n : 2 * n], in0=turns[:, 0:n], scalar1=FREQ_RATIO**n, scalar2=None,
                    op0=ALU.mult,
                )
                n *= 2

        def reduce_turns():
            low = turns[:, 0:REDUCED]
            for source, shift in ((low, ROUND), (whole, -ROUND)):
                nc.gpsimd.tensor_scalar(
                    out=whole, in0=source, scalar1=1.0, scalar2=shift, op0=ALU.mult, op1=ALU.add
                )
            nc.gpsimd.tensor_tensor(out=low, in0=low, in1=whole, op=ALU.subtract)

        def fill_emb_sin():
            nc.scalar.activation(out=cos_t[:, 0:HALF_E], in_=turns, func=ACT.Sin, scale=2.0 * math.pi)

        def fill_emb_cos():
            nc.scalar.activation(out=abs_turns, in_=turns[:, 0:REDUCED], func=ACT.Abs)
            for first, magnitudes in ((REDUCED, turns[:, REDUCED:HALF_E]), (0, abs_turns)):
                nc.scalar.activation(
                    out=cos_t[:, HALF_E + first : HALF_E + first + REDUCED], in_=magnitudes, func=ACT.Sin,
                    scale=-2.0 * math.pi, bias=math.pi / 2.0,
                )

        def fill_sin(half, sign):
            nc.scalar.activation(out=sin_t[:, half], in_=cos_t[:, half], func=ACT.Sin, scale=sign)

        def fill_cos(half):
            nc.scalar.activation(out=cos_t[:, half], in_=cos_t[:, half], func=ACT.Sin, bias=math.pi / 2.0)

        first_half, second_half = slice(0, HALF_E), slice(HALF_E, E)
        table_steps = [
            (fill_emb_sin, ()),
            (fill_emb_cos, ()),
            (fill_sin, (first_half, -1.0)),
            (fill_sin, (second_half, 1.0)),
            (fill_cos, (first_half,)),
            (fill_cos, (second_half,)),
        ]

        with tc.tile_pool(name="head", bufs=1) as head:
            nc.vector.memset(vectors[:].bitcast(F32), 0.0)
            x_raw = []
            for m in range(TOKEN_TILES):
                x_raw.append(head.tile([P, D], BF16, name="x_raw%d" % m))
            def load_x(m):
                nc.sync.dma_start(out=x_raw[m][:], in_=x_rows[m * P : (m + 1) * P, :])
            load_x(0)
            for piece, vector in ((GAIN_PIECE, g1), (SHIFT_PIECE, be1), (BIAS_PIECE, bqkv)):
                nc.sync.dma_start(
                    out=vectors[piece : piece + vector.shape[0] // PIECE, :], in_=vector.rearrange("(r n) -> r n", n=PIECE)
                )
            load_slab(0, ROW_TILES)
            load_x(1)
            for slab in range(1, W_BUFS):
                load_slab(slab, 1)

            pos = head.tile([P, 1], F32)
            for first in range(0, P, POSITIONS):
                nc.gpsimd.iota(
                    pos[first : first + POSITIONS, :],
                    pattern=[[0, 1]],
                    base=0,
                    channel_multiplier=1,
                    allow_small_or_imprecise_dtypes=True,
                )
            nc.gpsimd.tensor_scalar(
                out=turns[:, 0:1], in0=pos[:], scalar1=1.0 / (2.0 * math.pi), scalar2=0.0,
                op0=ALU.mult, op1=ALU.add,
            )
            make_identity(nc, ident[:])
            minus_half = head.tile([P, 1], F32)
            nc.gpsimd.memset(minus_half[:], -0.5)
            table_load = head.tile([P, 1], F32)
            nc.scalar.activation(out=table_load[:], in_=pos[:], func=ACT.Sin, scale=1.0 / POSITIONS)
            double_turns(1, 256)
            nc.vector.tensor_copy(out=select[:], in_=ident[:, 0:PIECES])
            double_turns(256, HALF_E)
            reduce_turns()
            for step, args in table_steps[:EARLY_TABLE_STEPS]:
                step(*args)

            mean = []
            rstd = []

            def take_rstd(m, variance):
                rstd.append(head.tile([P, 1], F32, name="rstd%d" % m))
                nc.gpsimd.tensor_scalar(
                    out=rstd[m][:], in0=variance, scalar1=1.0, scalar2=EPS, op0=ALU.mult, op1=ALU.add
                )
                nc.gpsimd.tensor_tensor(out=rstd[m][:], in0=rstd[m][:], in1=minus_half[:], op=ALU.pow)

            def take_stats(m):
                stats = head.tile([P, D // 512, 6], F32, name="stats%d" % m)
                mean_var = head.tile([P, 2], F32, name="mean_var%d" % m)
                for j in range(D // 512):
                    nc.vector.bn_stats(out=stats[:, j, :], in_=x_raw[m][:, j * 512 : (j + 1) * 512])
                nc.vector.bn_aggr(out=mean_var[:], in_=stats[:].rearrange("p c s -> p (c s)"))
                mean.append(mean_var[:, 0:1])
                take_rstd(m, mean_var[:, 1:2])

            gain_banks = [spread_half(GAIN_PIECE + j * HALF_D // PIECE, psum_acc, "acc") for j in range(2)]
            shift_banks = [spread_half(SHIFT_PIECE + j * HALF_D // PIECE, psum_acc, "acc") for j in range(2)]
            for m in range(TOKEN_TILES):
                take_stats(m)
            for slab in range(SLABS_BEFORE_X):
                transpose_slab(slab)
            centred = [head.tile([P, D], F32, name="centred%d" % m) for m in range(TOKEN_TILES)]
            xn = [head.tile([P, D], BF16, name="xn%d" % m) for m in range(TOKEN_TILES)]
            grouped_x = head.tile([P, PASSES * TOKENS * PACK], BF16, align_bytes=64)
            dest_x = grouped_x[:].bitcast(F32).rearrange(
                "p (g m n u) -> p g m n u", g=PASSES, m=TOKEN_TILES, u=2
            )
            halves = [slice(0, HALF_D), slice(HALF_D, D)]
            for j, half in enumerate(halves):
                for m in range(TOKEN_TILES):
                    nc.vector.scalar_tensor_tensor(
                        out=centred[m][:, half], in0=x_raw[m][:, half], scalar=mean[m],
                        in1=gain_banks[j][:], op0=ALU.subtract, op1=ALU.mult,
                    )
            for j, half in enumerate(halves):
                for m in range(TOKEN_TILES):
                    nc.vector.scalar_tensor_tensor(
                        out=xn[m][:, half], in0=centred[m][:, half], scalar=rstd[m][:],
                        in1=shift_banks[j][:], op0=ALU.mult, op1=ALU.add,
                    )

            def transpose_x(j):
                for g in range(j * PASSES // 2, (j + 1) * PASSES // 2):
                    transpose_words(lambda m, u: every_second_word(xn[m][:], g, u), dest_x[:, g, :, :, :])

            transpose_x(0)
            transpose_slab(SLABS_BEFORE_X, between=lambda: transpose_x(1))
            for slab in range(QUANTISED_BEFORE_X):
                quantise_slab(slab)
            nc.vector.quantize_mx(out=x_codes[:].bitcast(FP8X4), scales=x_scales[:], in_=grouped_x[:])
            for slab in range(SLABS_BEFORE_X + 1, SLABS_AHEAD):
                transpose_slab(slab)
            for slab in range(QUANTISED_BEFORE_X, QUANTISE_AHEAD):
                quantise_slab(slab)

        rot = pools.enter_context(tc.tile_pool(name="rot", bufs=4))

        def add_bias(pair, m, dest, first=0, slabs=2):
            by_feature = dict(h=slabs, t=ROW_TILES)
            columns = slice(first * SLAB, (first + slabs) * SLAB)
            features = slice((2 * pair + first) * SLAB, (2 * pair + first + slabs) * SLAB)
            nc.vector.tensor_tensor(
                out=dest.rearrange("r (h p t) -> r h p t", **by_feature),
                in0=acc[pair, m][:, columns].rearrange("r (h t p) -> r h p t", **by_feature),
                in1=bias_bc[:, features].rearrange("r (h p t) -> r h p t", **by_feature),
                op=ALU.add,
            )

        def finish_v(pair, first=0, slabs=2):
            start = (2 * (pair - FIRST_V) + first) * SLAB
            for m in range(TOKEN_TILES):
                v_rows = rot.tile([P, BANK], F32, name="v_rows", bufs=6)
                add_bias(pair, m, v_rows[:, 0 : slabs * SLAB], first, slabs)
                nc.sync.dma_start(
                    out=out_rows[2][m * P : (m + 1) * P, start : start + slabs * SLAB],
                    in_=v_rows[:, 0 : slabs * SLAB],
                )

        def for_both_tiles(table):
            return table.unsqueeze(1).broadcast_to([P, TOKEN_TILES] + list(table.shape[1:]))

        def multiply_by_sin(rows, rot_rows, j):
            nc.vector.tensor_tensor(
                out=rot_rows[:].rearrange("r m (h j i) -> r m h j i", h=2, j=2)[:, :, :, j, :],
                in0=rows[:, :, j * HALF_E : (j + 1) * HALF_E].rearrange("r m (i h) -> r m h i", h=2),
                in1=for_both_tiles(sin_t[:].rearrange("r (h j i) -> r h j i", h=2, j=2)[:, :, j, :]),
                op=ALU.mult,
            )

        def multiply_by_cos(rows, j):
            span = slice(j * HALF_E, (j + 1) * HALF_E)
            nc.vector.tensor_tensor(
                out=rows[:, :, span], in0=rows[:, :, span], in1=for_both_tiles(cos_t[:, span]), op=ALU.mult
            )

        def add_rotated(which, rows, rot_rows, span):
            nc.vector.tensor_tensor(
                out=rows[:, :, span], in0=rows[:, :, span], in1=rot_rows[:, :, span],
                op=(ALU.add if which == 0 else ALU.subtract),
            )
            if span.stop == E:
                for m in range(TOKEN_TILES):
                    nc.sync.dma_start(out=out_rows[which][m * P : (m + 1) * P, :], in_=rows[:, m, :])

        def finish_q_or_k(pair):
            which, s = divmod(pair, PAIRS_PER_OUTPUT)
            if s == 0:
                q_rows[which] = rot.tile([P, TOKEN_TILES, E], F32, name="q_rows", bufs=2)
                mixed[which] = rot.tile([P, TOKEN_TILES, E], F32, name="mixed", bufs=1)
            for m in range(TOKEN_TILES):
                add_bias(pair, m, q_rows[which][:, m, s * BANK : (s + 1) * BANK])
            if s % 2 == 1:
                j = s // 2
                ready = slice(0, HALF_E // 2) if j == 0 else slice(HALF_E // 2, E)
                mix_queue.append((multiply_by_sin, (q_rows[which], mixed[which], j)))
                mix_queue.append((multiply_by_cos, (q_rows[which], j)))
                mix_queue.append((add_rotated, (which, q_rows[which], mixed[which], ready)))

        def finish(pair):
            if pair < FIRST_V:
                finish_q_or_k(pair)
            else:
                finish_v(pair)

        def mix(steps):
            for step, args in mix_queue[:steps]:
                step(*args)
            mix_queue[:] = mix_queue[steps:]

        def multiply(slab):
            pair, half = divmod(slab, 2)
            columns = slice(half * SLAB, (half + 1) * SLAB)
            for g in range(PASSES):
                features = slice(g * SLAB, (g + 1) * SLAB)
                for m in range(TOKEN_TILES):
                    if half == 0 and g == 0:
                        acc[pair, m] = psum_acc.tile([P, BANK], F32, name="acc", tag="acc")
                    tokens = slice(g * TOKENS + m * P, g * TOKENS + (m + 1) * P)
                    nc.tensor.matmul_mx(
                        out=acc[pair, m][:, columns],
                        lhsT=x_codes[:, tokens].bitcast(FP8X4),
                        lhsT_scale=x_scales[:, tokens],
                        rhs=w_codes[slab][:, features].bitcast(FP8X4),
                        rhs_scale=w_scales[slab][:, features],
                        start=(g == 0),
                        stop=(g == PASSES - 1),
                    )

        for slab in range(SLABS):
            multiply(slab)
            if slab in BIAS_AFTER:
                spread_bias(BIAS_AFTER.index(slab))
            if SLABS_AHEAD <= slab + AHEAD < SLABS:
                transpose_slab(slab + AHEAD)
            if slab + EARLY_TABLE_STEPS < len(table_steps):
                step, args = table_steps[slab + EARLY_TABLE_STEPS]
                step(*args)
            if slab > 0 and slab % 2 == 0:
                finish(slab // 2 - 1)
            if slab == SLABS - 1:
                finish_v(SLABS // 2 - 1, first=0, slabs=1)
            mix(MIX_STEPS)
            if slab + QUANTISE_AHEAD < SLABS:
                quantise_slab(slab + QUANTISE_AHEAD, 2 if slab + QUANTISE_AHEAD == SLABS - 1 else 1)
        finish_v(SLABS // 2 - 1, first=1, slabs=1)
